import numpy as np
import ml_dtypes


def mxq(x, axis, fmt="e4m3"):
    dtype, down = {"e4m3": (ml_dtypes.float8_e4m3fn, 7), "e5m2": (ml_dtypes.float8_e5m2, 14)}[fmt]
    v = np.moveaxis(np.asarray(x, np.float32).astype(ml_dtypes.bfloat16).astype(np.float64), axis, -1)
    blocks = v.reshape(v.shape[:-1] + (-1, 32))
    amax = np.abs(blocks).max(-1, keepdims=True)
    byte = np.maximum(np.where(amax > 0, np.frexp(amax)[1] - 1 + 127, 0) - down, 1)
    scale = np.exp2(byte - 127.0)
    codes = (blocks / scale).astype(np.float32).astype(dtype).astype(np.float64)
    return np.moveaxis((codes * scale).reshape(v.shape), -1, axis)


WIDE = False


def mx_kscale(k):
    if not WIDE:
        return np.ones(k)
    levels = np.array([10, -10, 5, -5, 0])
    a = np.random.permutation(np.resize(levels, k // 512 * 4)).reshape(k // 512, 4)
    idx = np.arange(k)
    return np.exp2(a[idx // 512, idx % 128 // 32])


BF16 = ml_dtypes.bfloat16


def bf(x):
    return np.asarray(x, np.float32).astype(BF16)


def f64(x):
    return np.asarray(x).astype(np.float64)


B, K, N = 1024, 2048, 2048
EPS = 1e-5
GELU_C = 0.7978845608


def setup_inputs():
    s = mx_kscale(K)
    return {"x": bf(np.random.standard_normal((B, K)) * s),
            "weight": bf(np.random.standard_normal((K, N)) * np.sqrt(2.0 / K) / s[:, None]),
            "bn_gamma": bf(np.random.uniform(0.5, 1.5, N)),
            "bn_beta": bf(np.random.standard_normal(N) * 0.1),
            "bn_mean": bf(np.random.standard_normal(N) * 0.1),
            "bn_var": bf(np.random.uniform(0.5, 1.5, N))}


def reference(x, weight, bn_gamma, bn_beta, bn_mean, bn_var):
    acc = mxq(f64(x), 1, "e4m3") @ mxq(f64(weight), 0, "e4m3")
    x_norm = (acc - f64(bn_mean)) / np.sqrt(f64(bn_var) + EPS)
    bn_out = f64(bn_gamma) * x_norm + f64(bn_beta)
    gelu = 0.5 * bn_out * (1.0 + np.tanh(GELU_C * (bn_out + 0.044715 * bn_out * bn_out * bn_out)))
    return np.maximum(gelu, 0.0)

@@ -1,0 +1,281 @@
+from contextlib import ExitStack
+
+import concourse.mybir as mybir
+from concourse.masks import make_identity
+
+FP8X4 = mybir.dt.float8_e4m3fn_x4
+BF16 = mybir.dt.bfloat16
+F32 = mybir.dt.float32
+U32 = mybir.dt.uint32
+U8 = mybir.dt.uint8
+ACT = mybir.ActivationFunctionType
+ALU = mybir.AluOpType
+
+P = 128
+B, K, N = 1024, 2048, 2048
+EPS = 1e-5
+FLOPS = 2 * B * K * N
+
+PASSES = K // 512
+ROW_TILES = B // P
+HALF = 512
+BLOCK = 512
+N_BLOCKS = N // BLOCK
+UNITS = 2 * N_BLOCKS
+PINNED = False
+
+
+def tile_modelnew_kernel(tc, x, weight, bn_gamma, bn_beta, bn_mean, bn_var, out):
+    nc = tc.nc
+    x_v = x.rearrange("(p t) k -> p t k", t=ROW_TILES)
+    out_v = out.rearrange("(p t) n -> p t n", t=ROW_TILES)
+
+    with ExitStack() as ctx:
+        const = ctx.enter_context(tc.tile_pool(name="const", bufs=1))
+        keep = ctx.enter_context(tc.tile_pool(name="keep", bufs=1))
+        wg_pool = ctx.enter_context(tc.tile_pool(name="wg_pool", bufs=3))
+        xg_pool = ctx.enter_context(tc.tile_pool(name="xg_pool", bufs=8))
+        g_pool = ctx.enter_context(tc.tile_pool(name="g_pool", bufs=8))
+        o_pool = ctx.enter_context(tc.tile_pool(name="o_pool", bufs=3))
+        ps_acc = ctx.enter_context(tc.psum_pool(name="ps_acc", bufs=4))
+        ps_tr = ctx.enter_context(tc.psum_pool(name="ps_tr", bufs=4))
+        if PINNED:
+            ctx.enter_context(tc.manual_schedule())
+
+        x_raw = [keep.tile([P, K], BF16, name="x_raw%d" % t) for t in range(ROW_TILES)]
+        w_raw = [keep.tile([P, 4 * PASSES, BLOCK], BF16, name="w_raw%d" % nb) for nb in range(N_BLOCKS)]
+        w_codes = keep.tile([P, PASSES, N], U32, name="w_codes", align_bytes=64)
+        w_scales = keep.tile([P, PASSES, N], U8, name="w_scales", align_bytes=64)
+        x_codes = keep.tile([P, PASSES, B], U32, name="x_codes", align_bytes=64)
+        x_scales = keep.tile([P, PASSES, B], U8, name="x_scales", align_bytes=64)
+
+        def load_x(t):
+            nc.sync.dma_start(out=x_raw[t][:], in_=x_v[:, t, :])
+
+        def load_w(nb):
+            for j in range(2 * PASSES):
+                rows = weight[256 * j : 256 * j + 256, BLOCK * nb : BLOCK * nb + BLOCK]
+                nc.sync.dma_start(
+                    out=w_raw[nb][:, 2 * j : 2 * j + 2, :],
+                    in_=rows.rearrange("(q e) n -> q e n", e=2),
+                )
+
+        p_rows = const.tile([P, P], BF16, name="p_rows")
+        nc.vector.memset(p_rows[:], 0.0)
+        for v, vec in enumerate((bn_gamma, bn_beta, bn_mean, bn_var)):
+            nc.scalar.dma_start(out=p_rows[16 * v : 16 * v + 16, :], in_=vec.rearrange("(r c) -> r c", c=P))
+        for t in range(4):
+            load_x(t)
+        load_w(0)
+        for t in range(4, 8):
+            load_x(t)
+        for nb in range(1, N_BLOCKS):
+            load_w(nb)
+
+        ident_b = const.tile([P, P], BF16, name="ident_b")
+        make_identity(nc, ident_b[:])
+        ident_f = const.tile([P, P], F32, name="ident_f")
+        make_identity(nc, ident_f[:])
+
+        p_cols_ps = ps_acc.tile([P, P], BF16, name="p_cols_ps", tag="acc")
+        nc.tensor.transpose(p_cols_ps[:], p_rows[:], ident_b[:])
+        p_cols = const.tile([P, 64], F32, name="p_cols")
+        nc.vector.tensor_copy(out=p_cols[:], in_=p_cols_ps[:, 0:64])
+        var_eps = const.tile([P, 16], F32, name="var_eps")
+        nc.vector.tensor_scalar_add(var_eps[:], p_cols[:, 48:64], EPS)
+        std = const.tile([P, 16], F32, name="std")
+        nc.scalar.sqrt(std[:], var_eps[:])
+        rstd = const.tile([P, 16], F32, name="rstd")
+        nc.vector.reciprocal(rstd[:], std[:])
+        s_col = const.tile([P, 16], F32, name="s_col")
+        nc.vector.tensor_mul(s_col[:], p_cols[:, 0:16], rstd[:])
+        mean_s = const.tile([P, 16], F32, name="mean_s")
+        nc.vector.tensor_mul(mean_s[:], p_cols[:, 32:48], s_col[:])
+        t_col = const.tile([P, 16], F32, name="t_col")
+        nc.vector.tensor_sub(t_col[:], p_cols[:, 16:32], mean_s[:])
+
+        xt_tiles = {}
+        xg_tiles = {}
+        wg_tiles = {}
+        acc_tiles = {}
+        g_tiles = {}
+        tb_tiles = {}
+        o_tiles = {}
+
+        def XT(pair, g):
+            xt = ps_tr.tile([P, 2, 256], F32, name="xt", tag="tr")
+            for u in range(2):
+                for i in range(2):
+                    words = x_raw[2 * pair + i][:].bitcast(F32)
+                    j = 2 * g + u
+                    nc.tensor.transpose(xt[:, u, P * i : P * i + P], words[:, P * j : P * j + P], ident_f[:])
+            xt_tiles[(pair, g)] = xt
+
+        def XC(pair, g, eng):
+            xg = xg_pool.tile([P, 1024], BF16, name="xg", align_bytes=64)
+            dst = xg[:].bitcast(F32).rearrange("p (c u) -> p c u", u=2)
+            src = xt_tiles[(pair, g)][:].rearrange("p u c -> p c u")
+            if eng == "S":
+                nc.scalar.copy(out=dst, in_=src)
+            else:
+                nc.vector.tensor_copy(out=dst, in_=src)
+            xg_tiles[(pair, g)] = xg
+
+        def XQ(pair, g):
+            cols = slice(256 * pair, 256 * pair + 256)
+            nc.vector.quantize_mx(
+                out=x_codes[:, g, cols].bitcast(FP8X4), scales=x_scales[:, g, cols], in_=xg_tiles[(pair, g)][:]
+            )
+
+        def WR(nb, g, v_cols):
+            wg = wg_pool.tile([P, BLOCK, 4], BF16, name="wg", align_bytes=64)
+            for eng, c0, c1 in (("V", 0, v_cols), ("S", v_cols, BLOCK)):
+                if c0 == c1:
+                    continue
+                dst = wg[:, c0:c1, :].rearrange("p (c i) t -> p c t i", i=4)
+                src = w_raw[nb][:, 4 * g : 4 * g + 4, c0:c1].rearrange("p t (c i) -> p c t i", i=4)
+                if eng == "S":
+                    nc.scalar.copy(out=dst, in_=src)
+                else:
+                    nc.vector.tensor_copy(out=dst, in_=src)
+            wg_tiles[(nb, g)] = wg
+
+        def WQ(nb, g):
+            cols = slice(BLOCK * nb, BLOCK * nb + BLOCK)
+            nc.vector.quantize_mx(
+                out=w_codes[:, g, cols].bitcast(FP8X4),
+                scales=w_scales[:, g, cols],
+                in_=wg_tiles[(nb, g)][:].rearrange("p n t -> p (n t)"),
+            )
+
+        def mx_pass(u, i, g):
+            nb, h = divmod(u, 2)
+            if g == 0:
+                acc_tiles[(u, i)] = ps_acc.tile([P, HALF], F32, name="acc", tag="acc")
+            nt = 4 * nb + i
+            n_cols = slice(P * nt, P * nt + P)
+            b_cols = slice(HALF * h, HALF * h + HALF)
+            nc.tensor.matmul_mx(
+                out=acc_tiles[(u, i)][:],
+                lhsT=w_codes[:, g, n_cols].bitcast(FP8X4),
+                lhsT_scale=w_scales[:, g, n_cols],
+                rhs=x_codes[:, g, b_cols].bitcast(FP8X4),
+                rhs_scale=x_scales[:, g, b_cols],
+                start=(g == 0),
+                stop=(g == PASSES - 1),
+            )
+
+        def MX(u, i):
+            for g in range(PASSES):
+                mx_pass(u, i, g)
+
+        def GE(u, i):
+            nt = 4 * (u // 2) + i
+            g_t = g_pool.tile([P, HALF], F32, name="g_t")
+            nc.scalar.activation(
+                out=g_t[:], in_=acc_tiles[(u, i)][:],
+                func=(ACT.Gelu_apprx_tanh if i % 2 == 0 else ACT.Relu),
+                bias=t_col[:, nt : nt + 1], scale=s_col[:, nt : nt + 1],
+            )
+            g_tiles[(u, i)] = g_t
+
+        def TB(u, i):
+            tb = ps_tr.tile([P, 4, P], F32, name="tb", tag="tr")
+            for tt in range(4):
+                nc.tensor.transpose(tb[:, tt, :], g_tiles[(u, i)][:, P * tt : P * tt + P], ident_f[:])
+            tb_tiles[(u, i)] = tb
+
+        def RX(u, i):
+            if i == 0:
+                o_tiles[u] = o_pool.tile([P, 4, BLOCK], F32, name="o_sb")
+            dst = o_tiles[u][:, :, P * i : P * i + P]
+            if i % 2 == 0:
+                nc.vector.tensor_scalar(dst, tb_tiles[(u, i)][:], 0.0, 0.0, op0=ALU.max, op1=ALU.add)
+            else:
+                nc.scalar.activation(out=dst, in_=tb_tiles[(u, i)][:], func=ACT.Gelu_apprx_tanh)
+
+        def ST(u):
+            nb, h = divmod(u, 2)
+            nc.sync.dma_start(out=out_v[:, 4 * h : 4 * h + 4, BLOCK * nb : BLOCK * nb + BLOCK], in_=o_tiles[u][:])
+
+        for g in range(4):
+            XT(0, g)
+        for g in range(4):
+            XC(0, g, "S")
+            XQ(0, g)
+        for g in range(4):
+            XT(1, g)
+        XC(1, 0, "S")
+        XQ(1, 0)
+        XC(1, 1, "S")
+        XQ(1, 1)
+        WR(0, 0, BLOCK)
+        XC(1, 2, "S")
+        XQ(1, 2)
+        WQ(0, 0)
+        XC(1, 3, "S")
+        XQ(1, 3)
+        for i in range(4):
+            mx_pass(0, i, 0)
+        for g in range(1, 4):
+            WR(0, g, 256)
+            WQ(0, g)
+            for i in range(4):
+                mx_pass(0, i, g)
+        for g in range(4):
+            XT(2, g)
+        for g in range(4):
+            XT(3, g)
+        GE(0, 0)
+        XC(2, 0, "V")
+        XC(2, 1, "S")
+        XQ(2, 0)
+        XC(2, 2, "V")
+        XQ(2, 1)
+        GE(0, 1)
+        XC(2, 3, "S")
+        XQ(2, 2)
+        XQ(2, 3)
+        XC(3, 0, "S")
+        XC(3, 1, "V")
+        XQ(3, 0)
+        XC(3, 2, "S")
+        XQ(3, 1)
+        XC(3, 3, "S")
+        XQ(3, 2)
+        XQ(3, 3)
+        MX(1, 0)
+        MX(1, 1)
+        GE(0, 2)
+        GE(0, 3)
+        MX(1, 2)
+        MX(1, 3)
+        for i in range(4):
+            TB(0, i)
+        for g in range(4):
+            WR(1, g, 256)
+            GE(1, g)
+            WQ(1, g)
+        for i in range(4):
+            RX(0, i)
+        ST(0)
+        for u in range(2, UNITS):
+            nb, h = divmod(u, 2)
+            for i in range(4):
+                MX(u, i)
+                GE(u, i)
+            if nb + 1 < N_BLOCKS:
+                WR(nb + 1, 2 * h, BLOCK)
+                WR(nb + 1, 2 * h + 1, BLOCK)
+                WQ(nb + 1, 2 * h)
+                WQ(nb + 1, 2 * h + 1)
+            for i in range(4):
+                TB(u - 1, i)
+            for i in range(4):
+                RX(u - 1, i)
+            ST(u - 1)
+        for i in range(4):
+            TB(UNITS - 1, i)
+        for i in range(4):
+            RX(UNITS - 1, i)
+        ST(UNITS - 1)

@@ -22,7 +22,7 @@ HALF = 512
 BLOCK = 512
 N_BLOCKS = N // BLOCK
 UNITS = 2 * N_BLOCKS
-PINNED = False
+PINNED = True
 
 
 def tile_modelnew_kernel(tc, x, weight, bn_gamma, bn_beta, bn_mean, bn_var, out):
@@ -52,8 +52,8 @@ def tile_modelnew_kernel(tc, x, weight, bn_gamma, bn_beta, bn_mean, bn_var, out)
         def load_x(t):
             nc.sync.dma_start(out=x_raw[t][:], in_=x_v[:, t, :])
 
-        def load_w(nb):
-            for j in range(2 * PASSES):
+        def load_w(nb, g):
+            for j in (2 * g, 2 * g + 1):
                 rows = weight[256 * j : 256 * j + 256, BLOCK * nb : BLOCK * nb + BLOCK]
                 nc.sync.dma_start(
                     out=w_raw[nb][:, 2 * j : 2 * j + 2, :],
@@ -64,35 +64,67 @@ def tile_modelnew_kernel(tc, x, weight, bn_gamma, bn_beta, bn_mean, bn_var, out)
         nc.vector.memset(p_rows[:], 0.0)
         for v, vec in enumerate((bn_gamma, bn_beta, bn_mean, bn_var)):
             nc.scalar.dma_start(out=p_rows[16 * v : 16 * v + 16, :], in_=vec.rearrange("(r c) -> r c", c=P))
-        for t in range(4):
-            load_x(t)
-        load_w(0)
-        for t in range(4, 8):
-            load_x(t)
-        for nb in range(1, N_BLOCKS):
-            load_w(nb)
+        load_x(0)
+        load_x(1)
+        load_x(2)
+        load_x(3)
+        load_w(0, 0)
+        load_w(0, 1)
+        load_w(0, 2)
+        load_w(0, 3)
+        load_x(4)
+        load_x(5)
+        load_x(6)
+        load_x(7)
+        load_w(1, 0)
+        load_w(1, 1)
+        load_w(1, 2)
+        load_w(1, 3)
+        load_w(2, 0)
+        load_w(2, 1)
+        load_w(2, 2)
+        load_w(2, 3)
+        load_w(3, 0)
+        load_w(3, 1)
+        load_w(3, 2)
+        load_w(3, 3)
 
-        ident_b = const.tile([P, P], BF16, name="ident_b")
-        make_identity(nc, ident_b[:])
         ident_f = const.tile([P, P], F32, name="ident_f")
         make_identity(nc, ident_f[:])
+        ident_b = const.tile([P, P], BF16, name="ident_b")
+        make_identity(nc, ident_b[:])
+        minus_half = const.tile([P, 16], F32, name="minus_half")
+        nc.gpsimd.memset(minus_half[:], -0.5)
 
-        p_cols_ps = ps_acc.tile([P, P], BF16, name="p_cols_ps", tag="acc")
-        nc.tensor.transpose(p_cols_ps[:], p_rows[:], ident_b[:])
-        p_cols = const.tile([P, 64], F32, name="p_cols")
-        nc.vector.tensor_copy(out=p_cols[:], in_=p_cols_ps[:, 0:64])
+        p_cols = const.tile([P, 48], F32, name="p_cols")
         var_eps = const.tile([P, 16], F32, name="var_eps")
-        nc.vector.tensor_scalar_add(var_eps[:], p_cols[:, 48:64], EPS)
-        std = const.tile([P, 16], F32, name="std")
-        nc.scalar.sqrt(std[:], var_eps[:])
         rstd = const.tile([P, 16], F32, name="rstd")
-        nc.vector.reciprocal(rstd[:], std[:])
         s_col = const.tile([P, 16], F32, name="s_col")
-        nc.vector.tensor_mul(s_col[:], p_cols[:, 0:16], rstd[:])
         mean_s = const.tile([P, 16], F32, name="mean_s")
-        nc.vector.tensor_mul(mean_s[:], p_cols[:, 32:48], s_col[:])
         t_col = const.tile([P, 16], F32, name="t_col")
-        nc.vector.tensor_sub(t_col[:], p_cols[:, 16:32], mean_s[:])
+        warm_in = const.tile([P, 1], F32, name="warm_in")
+        warm_out = const.tile([P, 1], F32, name="warm_out")
+        nc.vector.memset(warm_in[:], 0.0)
+        par_tiles = {}
+
+        def WARM():
+            nc.scalar.activation(out=warm_out[:], in_=warm_in[:], func=ACT.Gelu_apprx_tanh)
+
+        def PT():
+            par_tiles["ps"] = ps_acc.tile([P, P], BF16, name="p_cols_ps", tag="acc")
+            nc.tensor.transpose(par_tiles["ps"][:], p_rows[:], ident_b[:])
+
+        def PC():
+            nc.vector.tensor_copy(out=p_cols[:], in_=par_tiles["ps"][:, 0:48])
+            nc.vector.tensor_scalar_add(var_eps[:], par_tiles["ps"][:, 48:64], EPS)
+
+        def PW():
+            nc.gpsimd.tensor_tensor(out=rstd[:], in0=var_eps[:], in1=minus_half[:], op=ALU.pow)
+
+        def STt():
+            nc.vector.tensor_mul(s_col[:], p_cols[:, 0:16], rstd[:])
+            nc.vector.tensor_mul(mean_s[:], p_cols[:, 32:48], s_col[:])
+            nc.vector.tensor_sub(t_col[:], p_cols[:, 16:32], mean_s[:])
 
         xt_tiles = {}
         xg_tiles = {}
@@ -127,18 +159,16 @@ def tile_modelnew_kernel(tc, x, weight, bn_gamma, bn_beta, bn_mean, bn_var, out)
                 out=x_codes[:, g, cols].bitcast(FP8X4), scales=x_scales[:, g, cols], in_=xg_tiles[(pair, g)][:]
             )
 
-        def WR(nb, g, v_cols):
-            wg = wg_pool.tile([P, BLOCK, 4], BF16, name="wg", align_bytes=64)
-            for eng, c0, c1 in (("V", 0, v_cols), ("S", v_cols, BLOCK)):
-                if c0 == c1:
-                    continue
-                dst = wg[:, c0:c1, :].rearrange("p (c i) t -> p c t i", i=4)
-                src = w_raw[nb][:, 4 * g : 4 * g + 4, c0:c1].rearrange("p t (c i) -> p c t i", i=4)
-                if eng == "S":
-                    nc.scalar.copy(out=dst, in_=src)
-                else:
-                    nc.vector.tensor_copy(out=dst, in_=src)
-            wg_tiles[(nb, g)] = wg
+        def WR(nb, g, eng, c0, c1):
+            if (nb, g) not in wg_tiles:
+                wg_tiles[(nb, g)] = wg_pool.tile([P, BLOCK, 4], BF16, name="wg", align_bytes=64)
+            wg = wg_tiles[(nb, g)]
+            dst = wg[:, c0:c1, :].rearrange("p (c i) t -> p c t i", i=4)
+            src = w_raw[nb][:, 4 * g : 4 * g + 4, c0:c1].rearrange("p t (c i) -> p c t i", i=4)
+            if eng == "S":
+                nc.scalar.copy(out=dst, in_=src)
+            else:
+                nc.vector.tensor_copy(out=dst, in_=src)
 
         def WQ(nb, g):
             cols = slice(BLOCK * nb, BLOCK * nb + BLOCK)
@@ -169,6 +199,10 @@ def tile_modelnew_kernel(tc, x, weight, bn_gamma, bn_beta, bn_mean, bn_var, out)
             for g in range(PASSES):
                 mx_pass(u, i, g)
 
+        def MXg(u, g):
+            for i in range(4):
+                mx_pass(u, i, g)
+
         def GE(u, i):
             nt = 4 * (u // 2) + i
             g_t = g_pool.tile([P, HALF], F32, name="g_t")
@@ -186,7 +220,7 @@ def tile_modelnew_kernel(tc, x, weight, bn_gamma, bn_beta, bn_mean, bn_var, out)
             tb_tiles[(u, i)] = tb
 
         def RX(u, i):
-            if i == 0:
+            if u not in o_tiles:
                 o_tiles[u] = o_pool.tile([P, 4, BLOCK], F32, name="o_sb")
             dst = o_tiles[u][:, :, P * i : P * i + P]
             if i % 2 == 0:
@@ -194,88 +228,331 @@ def tile_modelnew_kernel(tc, x, weight, bn_gamma, bn_beta, bn_mean, bn_var, out)
             else:
                 nc.scalar.activation(out=dst, in_=tb_tiles[(u, i)][:], func=ACT.Gelu_apprx_tanh)
 
-        def ST(u):
+        def ST(u, i0, i1):
             nb, h = divmod(u, 2)
-            nc.sync.dma_start(out=out_v[:, 4 * h : 4 * h + 4, BLOCK * nb : BLOCK * nb + BLOCK], in_=o_tiles[u][:])
+            nc.sync.dma_start(
+                out=out_v[:, 4 * h : 4 * h + 4, BLOCK * nb + P * i0 : BLOCK * nb + P * i1],
+                in_=o_tiles[u][:, :, P * i0 : P * i1],
+            )
 
-        for g in range(4):
-            XT(0, g)
-        for g in range(4):
-            XC(0, g, "S")
-            XQ(0, g)
-        for g in range(4):
-            XT(1, g)
+        WARM()
+        XT(0, 0)
+        XT(0, 1)
+        XC(0, 0, "S")
+        XT(0, 2)
+        XC(0, 1, "S")
+        XQ(0, 0)
+        XT(0, 3)
+        XC(0, 2, "S")
+        XQ(0, 1)
+        PT()
+        XC(0, 3, "S")
+        XT(1, 0)
+        XQ(0, 2)
+        XT(1, 1)
+        XQ(0, 3)
         XC(1, 0, "S")
-        XQ(1, 0)
+        PC()
+        XT(1, 2)
         XC(1, 1, "S")
-        XQ(1, 1)
-        WR(0, 0, BLOCK)
+        PW()
+        XQ(1, 0)
+        XT(1, 3)
         XC(1, 2, "S")
+        XQ(1, 1)
+        WR(0, 0, "V", 0, 512)
+        XC(1, 3, "S")
+        WR(0, 1, "S", 256, 512)
         XQ(1, 2)
         WQ(0, 0)
-        XC(1, 3, "S")
+        WR(0, 2, "S", 256, 512)
         XQ(1, 3)
-        for i in range(4):
-            mx_pass(0, i, 0)
-        for g in range(1, 4):
-            WR(0, g, 256)
-            WQ(0, g)
-            for i in range(4):
-                mx_pass(0, i, g)
-        for g in range(4):
-            XT(2, g)
-        for g in range(4):
-            XT(3, g)
-        GE(0, 0)
+        WR(0, 1, "V", 0, 256)
+        mx_pass(0, 0, 0)
+        mx_pass(0, 1, 0)
+        WQ(0, 1)
+        mx_pass(0, 2, 0)
+        WR(0, 3, "S", 256, 512)
+        mx_pass(0, 3, 0)
+        WR(0, 2, "V", 0, 256)
+        mx_pass(0, 0, 1)
+        mx_pass(0, 1, 1)
+        WQ(0, 2)
+        mx_pass(0, 2, 1)
+        mx_pass(0, 3, 1)
+        WR(0, 3, "V", 0, 256)
+        mx_pass(0, 0, 2)
+        mx_pass(0, 1, 2)
+        WQ(0, 3)
+        mx_pass(0, 2, 2)
+        mx_pass(0, 3, 2)
+        STt()
+        XT(2, 0)
+        XT(2, 1)
         XC(2, 0, "V")
+        XT(2, 2)
         XC(2, 1, "S")
+        XT(2, 3)
         XQ(2, 0)
         XC(2, 2, "V")
-        XQ(2, 1)
-        GE(0, 1)
         XC(2, 3, "S")
+        mx_pass(0, 0, 3)
+        mx_pass(0, 1, 3)
+        XQ(2, 1)
+        GE(0, 0)
+        mx_pass(0, 2, 3)
         XQ(2, 2)
+        mx_pass(0, 3, 3)
         XQ(2, 3)
-        XC(3, 0, "S")
-        XC(3, 1, "V")
+        GE(0, 1)
+        XT(3, 0)
+        XT(3, 1)
+        XC(3, 0, "V")
+        XT(3, 2)
+        XC(3, 1, "S")
+        XT(3, 3)
         XQ(3, 0)
-        XC(3, 2, "S")
-        XQ(3, 1)
+        XC(3, 2, "V")
         XC(3, 3, "S")
+        mx_pass(1, 0, 0)
+        XQ(3, 1)
+        GE(0, 2)
         XQ(3, 2)
         XQ(3, 3)
-        MX(1, 0)
-        MX(1, 1)
-        GE(0, 2)
+        mx_pass(1, 0, 1)
         GE(0, 3)
-        MX(1, 2)
-        MX(1, 3)
-        for i in range(4):
-            TB(0, i)
-        for g in range(4):
-            WR(1, g, 256)
-            GE(1, g)
-            WQ(1, g)
-        for i in range(4):
-            RX(0, i)
-        ST(0)
-        for u in range(2, UNITS):
-            nb, h = divmod(u, 2)
-            for i in range(4):
-                MX(u, i)
-                GE(u, i)
-            if nb + 1 < N_BLOCKS:
-                WR(nb + 1, 2 * h, BLOCK)
-                WR(nb + 1, 2 * h + 1, BLOCK)
-                WQ(nb + 1, 2 * h)
-                WQ(nb + 1, 2 * h + 1)
-            for i in range(4):
-                TB(u - 1, i)
-            for i in range(4):
-                RX(u - 1, i)
-            ST(u - 1)
-        for i in range(4):
-            TB(UNITS - 1, i)
-        for i in range(4):
-            RX(UNITS - 1, i)
-        ST(UNITS - 1)
+        WR(1, 0, "V", 0, 512)
+        mx_pass(1, 0, 2)
+        mx_pass(1, 0, 3)
+        WR(1, 1, "S", 0, 512)
+        mx_pass(1, 1, 0)
+        mx_pass(1, 1, 1)
+        mx_pass(1, 1, 2)
+        WQ(1, 0)
+        mx_pass(1, 1, 3)
+        mx_pass(1, 2, 0)
+        WR(1, 2, "V", 0, 512)
+        mx_pass(1, 2, 1)
+        mx_pass(1, 2, 2)
+        GE(1, 0)
+        mx_pass(1, 2, 3)
+        mx_pass(1, 3, 0)
+        WQ(1, 1)
+        mx_pass(1, 3, 1)
+        GE(1, 1)
+        mx_pass(1, 3, 2)
+        WR(1, 3, "V", 0, 512)
+        mx_pass(1, 3, 3)
+        GE(1, 2)
+        TB(0, 0)
+        GE(1, 3)
+        TB(0, 1)
+        WQ(1, 2)
+        TB(0, 2)
+        RX(0, 1)
+        TB(0, 3)
+        WQ(1, 3)
+        mx_pass(2, 0, 0)
+        RX(0, 3)
+        mx_pass(2, 0, 1)
+        RX(0, 0)
+        mx_pass(2, 0, 2)
+        mx_pass(2, 0, 3)
+        RX(0, 2)
+        mx_pass(2, 1, 0)
+        GE(2, 0)
+        mx_pass(2, 1, 1)
+        WR(2, 0, "V", 0, 512)
+        mx_pass(2, 1, 2)
+        ST(0, 0, 4)
+        mx_pass(2, 1, 3)
+        mx_pass(2, 2, 0)
+        GE(2, 1)
+        mx_pass(2, 2, 1)
+        WR(2, 1, "V", 0, 512)
+        mx_pass(2, 2, 2)
+        mx_pass(2, 2, 3)
+        mx_pass(2, 3, 0)
+        GE(2, 2)
+        mx_pass(2, 3, 1)
+        WQ(2, 0)
+        mx_pass(2, 3, 2)
+        mx_pass(2, 3, 3)
+        WQ(2, 1)
+        GE(2, 3)
+        TB(1, 0)
+        TB(1, 1)
+        RX(1, 0)
+        TB(1, 2)
+        RX(1, 1)
+        TB(1, 3)
+        RX(1, 2)
+        RX(1, 3)
+        mx_pass(3, 0, 0)
+        WR(2, 2, "V", 0, 512)
+        mx_pass(3, 0, 1)
+        mx_pass(3, 0, 2)
+        ST(1, 0, 4)
+        mx_pass(3, 0, 3)
+        mx_pass(3, 1, 0)
+        GE(3, 0)
+        WR(2, 3, "V", 0, 512)
+        mx_pass(3, 1, 1)
+        mx_pass(3, 1, 2)
+        mx_pass(3, 1, 3)
+        mx_pass(3, 2, 0)
+        GE(3, 1)
+        WQ(2, 2)
+        mx_pass(3, 2, 1)
+        mx_pass(3, 2, 2)
+        WQ(2, 3)
+        mx_pass(3, 2, 3)
+        mx_pass(3, 3, 0)
+        GE(3, 2)
+        mx_pass(3, 3, 1)
+        mx_pass(3, 3, 2)
+        mx_pass(3, 3, 3)
+        GE(3, 3)
+        TB(2, 0)
+        TB(2, 1)
+        RX(2, 0)
+        TB(2, 2)
+        RX(2, 1)
+        TB(2, 3)
+        RX(2, 2)
+        RX(2, 3)
+        mx_pass(4, 0, 0)
+        WR(3, 0, "V", 0, 512)
+        mx_pass(4, 0, 1)
+        mx_pass(4, 0, 2)
+        ST(2, 0, 4)
+        mx_pass(4, 0, 3)
+        mx_pass(4, 1, 0)
+        GE(4, 0)
+        WR(3, 1, "V", 0, 512)
+        mx_pass(4, 1, 1)
+        mx_pass(4, 1, 2)
+        mx_pass(4, 1, 3)
+        mx_pass(4, 2, 0)
+        GE(4, 1)
+        WQ(3, 0)
+        mx_pass(4, 2, 1)
+        mx_pass(4, 2, 2)
+        WQ(3, 1)
+        mx_pass(4, 2, 3)
+        mx_pass(4, 3, 0)
+        GE(4, 2)
+        mx_pass(4, 3, 1)
+        mx_pass(4, 3, 2)
+        mx_pass(4, 3, 3)
+        GE(4, 3)
+        TB(3, 0)
+        TB(3, 1)
+        RX(3, 0)
+        TB(3, 2)
+        RX(3, 1)
+        TB(3, 3)
+        RX(3, 2)
+        RX(3, 3)
+        mx_pass(5, 0, 0)
+        WR(3, 2, "V", 0, 512)
+        mx_pass(5, 0, 1)
+        mx_pass(5, 0, 2)
+        ST(3, 0, 4)
+        mx_pass(5, 0, 3)
+        mx_pass(5, 1, 0)
+        GE(5, 0)
+        WR(3, 3, "V", 0, 512)
+        mx_pass(5, 1, 1)
+        mx_pass(5, 1, 2)
+        mx_pass(5, 1, 3)
+        mx_pass(5, 2, 0)
+        GE(5, 1)
+        WQ(3, 2)
+        mx_pass(5, 2, 1)
+        mx_pass(5, 2, 2)
+        WQ(3, 3)
+        mx_pass(5, 2, 3)
+        mx_pass(5, 3, 0)
+        GE(5, 2)
+        mx_pass(5, 3, 1)
+        mx_pass(5, 3, 2)
+        mx_pass(5, 3, 3)
+        GE(5, 3)
+        TB(4, 0)
+        TB(4, 1)
+        RX(4, 0)
+        TB(4, 2)
+        RX(4, 1)
+        TB(4, 3)
+        RX(4, 2)
+        RX(4, 3)
+        mx_pass(6, 0, 0)
+        mx_pass(6, 0, 1)
+        mx_pass(6, 0, 2)
+        ST(4, 0, 4)
+        mx_pass(6, 0, 3)
+        mx_pass(6, 1, 0)
+        GE(6, 0)
+        mx_pass(6, 1, 1)
+        mx_pass(6, 1, 2)
+        mx_pass(6, 1, 3)
+        mx_pass(6, 2, 0)
+        GE(6, 1)
+        mx_pass(6, 2, 1)
+        mx_pass(6, 2, 2)
+        mx_pass(6, 2, 3)
+        mx_pass(6, 3, 0)
+        GE(6, 2)
+        mx_pass(6, 3, 1)
+        mx_pass(6, 3, 2)
+        mx_pass(6, 3, 3)
+        GE(6, 3)
+        TB(5, 0)
+        TB(5, 1)
+        RX(5, 0)
+        TB(5, 2)
+        RX(5, 1)
+        TB(5, 3)
+        RX(5, 2)
+        RX(5, 3)
+        mx_pass(7, 0, 0)
+        mx_pass(7, 0, 1)
+        mx_pass(7, 0, 2)
+        ST(5, 0, 4)
+        mx_pass(7, 0, 3)
+        mx_pass(7, 1, 0)
+        GE(7, 0)
+        mx_pass(7, 1, 1)
+        mx_pass(7, 1, 2)
+        mx_pass(7, 1, 3)
+        GE(7, 1)
+        TB(6, 0)
+        TB(6, 1)
+        RX(6, 0)
+        TB(6, 2)
+        RX(6, 1)
+        TB(6, 3)
+        RX(6, 2)
+        RX(6, 3)
+        mx_pass(7, 2, 0)
+        mx_pass(7, 2, 1)
+        mx_pass(7, 2, 2)
+        ST(6, 0, 4)
+        mx_pass(7, 2, 3)
+        mx_pass(7, 3, 0)
+        GE(7, 2)
+        mx_pass(7, 3, 1)
+        mx_pass(7, 3, 2)
+        mx_pass(7, 3, 3)
+        GE(7, 3)
+        TB(7, 0)
+        TB(7, 1)
+        RX(7, 0)
+        TB(7, 2)
+        RX(7, 1)
+        TB(7, 3)
+        RX(7, 2)
+        RX(7, 3)
+        ST(7, 0, 2)
+        ST(7, 2, 4)

@@ -42,15 +42,15 @@ def tile_modelnew_kernel(tc, x, weight, bn_gamma, bn_beta, bn_mean, bn_var, out)
         if PINNED:
             ctx.enter_context(tc.manual_schedule())
 
-        x_raw = [keep.tile([P, K], BF16, name="x_raw%d" % t) for t in range(ROW_TILES)]
+        x_raw = [keep.tile([P, 2, K], BF16, name="x_raw%d" % pair) for pair in range(ROW_TILES // 2)]
         w_raw = [keep.tile([P, 4 * PASSES, BLOCK], BF16, name="w_raw%d" % nb) for nb in range(N_BLOCKS)]
         w_codes = keep.tile([P, PASSES, N], U32, name="w_codes", align_bytes=64)
         w_scales = keep.tile([P, PASSES, N], U8, name="w_scales", align_bytes=64)
         x_codes = keep.tile([P, PASSES, B], U32, name="x_codes", align_bytes=64)
         x_scales = keep.tile([P, PASSES, B], U8, name="x_scales", align_bytes=64)
 
-        def load_x(t):
-            nc.sync.dma_start(out=x_raw[t][:], in_=x_v[:, t, :])
+        def load_x(pair):
+            nc.sync.dma_start(out=x_raw[pair][:], in_=x_v[:, 2 * pair : 2 * pair + 2, :])
 
         def load_w(nb, g):
             for j in (2 * g, 2 * g + 1):
@@ -66,16 +66,12 @@ def tile_modelnew_kernel(tc, x, weight, bn_gamma, bn_beta, bn_mean, bn_var, out)
             nc.scalar.dma_start(out=p_rows[16 * v : 16 * v + 16, :], in_=vec.rearrange("(r c) -> r c", c=P))
         load_x(0)
         load_x(1)
-        load_x(2)
-        load_x(3)
         load_w(0, 0)
         load_w(0, 1)
         load_w(0, 2)
         load_w(0, 3)
-        load_x(4)
-        load_x(5)
-        load_x(6)
-        load_x(7)
+        load_x(2)
+        load_x(3)
         load_w(1, 0)
         load_w(1, 1)
         load_w(1, 2)
@@ -138,7 +134,7 @@ def tile_modelnew_kernel(tc, x, weight, bn_gamma, bn_beta, bn_mean, bn_var, out)
             xt = ps_tr.tile([P, 2, 256], F32, name="xt", tag="tr")
             for u in range(2):
                 for i in range(2):
-                    words = x_raw[2 * pair + i][:].bitcast(F32)
+                    words = x_raw[pair][:, i, :].bitcast(F32)
                     j = 2 * g + u
                     nc.tensor.transpose(xt[:, u, P * i : P * i + P], words[:, P * j : P * j + P], ident_f[:])
             xt_tiles[(pair, g)] = xt
@@ -254,33 +250,33 @@ def tile_modelnew_kernel(tc, x, weight, bn_gamma, bn_beta, bn_mean, bn_var, out)
         XC(1, 0, "S")
         PC()
         XT(1, 2)
+        WR(0, 0, "V", 0, 512)
         XC(1, 1, "S")
         PW()
-        XQ(1, 0)
         XT(1, 3)
         XC(1, 2, "S")
-        XQ(1, 1)
-        WR(0, 0, "V", 0, 512)
+        XQ(1, 0)
         XC(1, 3, "S")
-        WR(0, 1, "S", 256, 512)
-        XQ(1, 2)
         WQ(0, 0)
-        WR(0, 2, "S", 256, 512)
-        XQ(1, 3)
-        WR(0, 1, "V", 0, 256)
+        WR(0, 1, "S", 192, 512)
+        XQ(1, 1)
+        WR(0, 1, "V", 0, 192)
         mx_pass(0, 0, 0)
+        XQ(1, 2)
         mx_pass(0, 1, 0)
-        WQ(0, 1)
+        WR(0, 2, "S", 192, 512)
         mx_pass(0, 2, 0)
-        WR(0, 3, "S", 256, 512)
+        WQ(0, 1)
         mx_pass(0, 3, 0)
-        WR(0, 2, "V", 0, 256)
+        XQ(1, 3)
+        WR(0, 2, "V", 0, 192)
         mx_pass(0, 0, 1)
         mx_pass(0, 1, 1)
+        WR(0, 3, "S", 192, 512)
         WQ(0, 2)
         mx_pass(0, 2, 1)
         mx_pass(0, 3, 1)
-        WR(0, 3, "V", 0, 256)
+        WR(0, 3, "V", 0, 192)
         mx_pass(0, 0, 2)
         mx_pass(0, 1, 2)
         WQ(0, 3)
@@ -312,11 +308,13 @@ def tile_modelnew_kernel(tc, x, weight, bn_gamma, bn_beta, bn_mean, bn_var, out)
         XC(3, 1, "S")
         XT(3, 3)
         XQ(3, 0)
+        TB(0, 0)
         XC(3, 2, "V")
         XC(3, 3, "S")
-        mx_pass(1, 0, 0)
+        TB(0, 1)
         XQ(3, 1)
         GE(0, 2)
+        mx_pass(1, 0, 0)
         XQ(3, 2)
         XQ(3, 3)
         mx_pass(1, 0, 1)
@@ -344,39 +342,37 @@ def tile_modelnew_kernel(tc, x, weight, bn_gamma, bn_beta, bn_mean, bn_var, out)
         WR(1, 3, "V", 0, 512)
         mx_pass(1, 3, 3)
         GE(1, 2)
-        TB(0, 0)
-        GE(1, 3)
-        TB(0, 1)
-        WQ(1, 2)
         TB(0, 2)
-        RX(0, 1)
+        GE(1, 3)
         TB(0, 3)
-        WQ(1, 3)
+        WQ(1, 2)
         mx_pass(2, 0, 0)
-        RX(0, 3)
+        RX(0, 1)
         mx_pass(2, 0, 1)
-        RX(0, 0)
+        WQ(1, 3)
         mx_pass(2, 0, 2)
+        RX(0, 3)
+        RX(0, 0)
         mx_pass(2, 0, 3)
         RX(0, 2)
         mx_pass(2, 1, 0)
         GE(2, 0)
         mx_pass(2, 1, 1)
-        WR(2, 0, "V", 0, 512)
         mx_pass(2, 1, 2)
-        ST(0, 0, 4)
+        WR(2, 0, "V", 0, 512)
         mx_pass(2, 1, 3)
         mx_pass(2, 2, 0)
         GE(2, 1)
         mx_pass(2, 2, 1)
-        WR(2, 1, "V", 0, 512)
+        ST(0, 0, 4)
         mx_pass(2, 2, 2)
+        WR(2, 1, "V", 0, 512)
         mx_pass(2, 2, 3)
         mx_pass(2, 3, 0)
         GE(2, 2)
         mx_pass(2, 3, 1)
-        WQ(2, 0)
         mx_pass(2, 3, 2)
+        WQ(2, 0)
         mx_pass(2, 3, 3)
         WQ(2, 1)
         GE(2, 3)
@@ -389,24 +385,24 @@ def tile_modelnew_kernel(tc, x, weight, bn_gamma, bn_beta, bn_mean, bn_var, out)
         RX(1, 2)
         RX(1, 3)
         mx_pass(3, 0, 0)
-        WR(2, 2, "V", 0, 512)
         mx_pass(3, 0, 1)
+        WR(2, 2, "V", 0, 512)
         mx_pass(3, 0, 2)
         ST(1, 0, 4)
         mx_pass(3, 0, 3)
         mx_pass(3, 1, 0)
         GE(3, 0)
-        WR(2, 3, "V", 0, 512)
         mx_pass(3, 1, 1)
+        WR(2, 3, "V", 0, 512)
         mx_pass(3, 1, 2)
         mx_pass(3, 1, 3)
         mx_pass(3, 2, 0)
         GE(3, 1)
-        WQ(2, 2)
         mx_pass(3, 2, 1)
+        WQ(2, 2)
         mx_pass(3, 2, 2)
-        WQ(2, 3)
         mx_pass(3, 2, 3)
+        WQ(2, 3)
         mx_pass(3, 3, 0)
         GE(3, 2)
         mx_pass(3, 3, 1)
@@ -521,12 +517,7 @@ def tile_modelnew_kernel(tc, x, weight, bn_gamma, bn_beta, bn_mean, bn_var, out)
         mx_pass(7, 0, 2)
         ST(5, 0, 4)
         mx_pass(7, 0, 3)
-        mx_pass(7, 1, 0)
         GE(7, 0)
-        mx_pass(7, 1, 1)
-        mx_pass(7, 1, 2)
-        mx_pass(7, 1, 3)
-        GE(7, 1)
         TB(6, 0)
         TB(6, 1)
         RX(6, 0)
@@ -535,24 +526,30 @@ def tile_modelnew_kernel(tc, x, weight, bn_gamma, bn_beta, bn_mean, bn_var, out)
         TB(6, 3)
         RX(6, 2)
         RX(6, 3)
+        mx_pass(7, 1, 0)
+        mx_pass(7, 1, 1)
+        mx_pass(7, 1, 2)
+        ST(6, 0, 4)
+        mx_pass(7, 1, 3)
         mx_pass(7, 2, 0)
+        GE(7, 1)
         mx_pass(7, 2, 1)
         mx_pass(7, 2, 2)
-        ST(6, 0, 4)
         mx_pass(7, 2, 3)
-        mx_pass(7, 3, 0)
         GE(7, 2)
-        mx_pass(7, 3, 1)
-        mx_pass(7, 3, 2)
-        mx_pass(7, 3, 3)
-        GE(7, 3)
         TB(7, 0)
         TB(7, 1)
         RX(7, 0)
-        TB(7, 2)
         RX(7, 1)
-        TB(7, 3)
-        RX(7, 2)
-        RX(7, 3)
+        mx_pass(7, 3, 0)
+        mx_pass(7, 3, 1)
+        mx_pass(7, 3, 2)
         ST(7, 0, 2)
-        ST(7, 2, 4)
+        mx_pass(7, 3, 3)
+        GE(7, 3)
+        TB(7, 2)
+        RX(7, 2)
+        TB(7, 3)
+        RX(7, 3)
+        ST(7, 2, 3)
+        ST(7, 3, 4)

@@ -11,18 +11,24 @@ U8 = mybir.dt.uint8
 ACT = mybir.ActivationFunctionType
 ALU = mybir.AluOpType
 
-P = 128
 B, K, N = 1024, 2048, 2048
 EPS = 1e-5
 FLOPS = 2 * B * K * N
 
-PASSES = K // 512
+P = 128
+PACK = 4
+PASSES = K // (P * PACK)
 ROW_TILES = B // P
-HALF = 512
-BLOCK = 512
+PAIRS = ROW_TILES // 2
+HALF_TILES = 4
+HALF = HALF_TILES * P
+COL_TILES = 4
+BLOCK = COL_TILES * P
 N_BLOCKS = N // BLOCK
 UNITS = 2 * N_BLOCKS
-PINNED = True
+LAST = UNITS - 1
+SHARED_BLOCKS = 2
+VECTOR_COLS = BLOCK // 2
 
 
 def tile_modelnew_kernel(tc, x, weight, bn_gamma, bn_beta, bn_mean, bn_var, out):
@@ -34,16 +40,15 @@ def tile_modelnew_kernel(tc, x, weight, bn_gamma, bn_beta, bn_mean, bn_var, out)
         const = ctx.enter_context(tc.tile_pool(name="const", bufs=1))
         keep = ctx.enter_context(tc.tile_pool(name="keep", bufs=1))
         wg_pool = ctx.enter_context(tc.tile_pool(name="wg_pool", bufs=3))
-        xg_pool = ctx.enter_context(tc.tile_pool(name="xg_pool", bufs=8))
-        g_pool = ctx.enter_context(tc.tile_pool(name="g_pool", bufs=8))
+        xg_pool = ctx.enter_context(tc.tile_pool(name="xg_pool", bufs=2 * PASSES))
+        g_pool = ctx.enter_context(tc.tile_pool(name="g_pool", bufs=2 * COL_TILES))
         o_pool = ctx.enter_context(tc.tile_pool(name="o_pool", bufs=3))
         ps_acc = ctx.enter_context(tc.psum_pool(name="ps_acc", bufs=4))
         ps_tr = ctx.enter_context(tc.psum_pool(name="ps_tr", bufs=4))
-        if PINNED:
-            ctx.enter_context(tc.manual_schedule())
+        ctx.enter_context(tc.manual_schedule())
 
-        x_raw = [keep.tile([P, 2, K], BF16, name="x_raw%d" % pair) for pair in range(ROW_TILES // 2)]
-        w_raw = [keep.tile([P, 4 * PASSES, BLOCK], BF16, name="w_raw%d" % nb) for nb in range(N_BLOCKS)]
+        x_raw = [keep.tile([P, 2, K], BF16, name="x_raw%d" % pair) for pair in range(PAIRS)]
+        w_raw = [keep.tile([P, PACK * PASSES, BLOCK], BF16, name="w_raw%d" % nb) for nb in range(N_BLOCKS)]
         w_codes = keep.tile([P, PASSES, N], U32, name="w_codes", align_bytes=64)
         w_scales = keep.tile([P, PASSES, N], U8, name="w_scales", align_bytes=64)
         x_codes = keep.tile([P, PASSES, B], U32, name="x_codes", align_bytes=64)
@@ -52,8 +57,8 @@ def tile_modelnew_kernel(tc, x, weight, bn_gamma, bn_beta, bn_mean, bn_var, out)
         def load_x(pair):
             nc.sync.dma_start(out=x_raw[pair][:], in_=x_v[:, 2 * pair : 2 * pair + 2, :])
 
-        def load_w(nb, g):
-            for j in (2 * g, 2 * g + 1):
+        def load_w(nb):
+            for j in range(2 * PASSES):
                 rows = weight[256 * j : 256 * j + 256, BLOCK * nb : BLOCK * nb + BLOCK]
                 nc.sync.dma_start(
                     out=w_raw[nb][:, 2 * j : 2 * j + 2, :],
@@ -66,24 +71,11 @@ def tile_modelnew_kernel(tc, x, weight, bn_gamma, bn_beta, bn_mean, bn_var, out)
             nc.scalar.dma_start(out=p_rows[16 * v : 16 * v + 16, :], in_=vec.rearrange("(r c) -> r c", c=P))
         load_x(0)
         load_x(1)
-        load_w(0, 0)
-        load_w(0, 1)
-        load_w(0, 2)
-        load_w(0, 3)
+        load_w(0)
         load_x(2)
         load_x(3)
-        load_w(1, 0)
-        load_w(1, 1)
-        load_w(1, 2)
-        load_w(1, 3)
-        load_w(2, 0)
-        load_w(2, 1)
-        load_w(2, 2)
-        load_w(2, 3)
-        load_w(3, 0)
-        load_w(3, 1)
-        load_w(3, 2)
-        load_w(3, 3)
+        for nb in range(1, N_BLOCKS):
+            load_w(nb)
 
         ident_f = const.tile([P, P], F32, name="ident_f")
         make_identity(nc, ident_f[:])
@@ -101,88 +93,80 @@ def tile_modelnew_kernel(tc, x, weight, bn_gamma, bn_beta, bn_mean, bn_var, out)
         warm_in = const.tile([P, 1], F32, name="warm_in")
         warm_out = const.tile([P, 1], F32, name="warm_out")
         nc.vector.memset(warm_in[:], 0.0)
-        par_tiles = {}
+        tiles = {}
 
-        def WARM():
+        def load_gelu_table():
             nc.scalar.activation(out=warm_out[:], in_=warm_in[:], func=ACT.Gelu_apprx_tanh)
 
-        def PT():
-            par_tiles["ps"] = ps_acc.tile([P, P], BF16, name="p_cols_ps", tag="acc")
-            nc.tensor.transpose(par_tiles["ps"][:], p_rows[:], ident_b[:])
+        def transpose_params():
+            tiles["params"] = ps_acc.tile([P, P], BF16, name="params", tag="acc")
+            nc.tensor.transpose(tiles["params"][:], p_rows[:], ident_b[:])
 
-        def PC():
-            nc.vector.tensor_copy(out=p_cols[:], in_=par_tiles["ps"][:, 0:48])
-            nc.vector.tensor_scalar_add(var_eps[:], par_tiles["ps"][:, 48:64], EPS)
-
-        def PW():
+        def inverse_std():
+            nc.vector.tensor_copy(out=p_cols[:], in_=tiles["params"][:, 0:48])
+            nc.vector.tensor_scalar_add(var_eps[:], tiles["params"][:, 48:64], EPS)
             nc.gpsimd.tensor_tensor(out=rstd[:], in0=var_eps[:], in1=minus_half[:], op=ALU.pow)
 
-        def STt():
+        def scale_and_shift():
             nc.vector.tensor_mul(s_col[:], p_cols[:, 0:16], rstd[:])
             nc.vector.tensor_mul(mean_s[:], p_cols[:, 32:48], s_col[:])
             nc.vector.tensor_sub(t_col[:], p_cols[:, 16:32], mean_s[:])
 
-        xt_tiles = {}
-        xg_tiles = {}
-        wg_tiles = {}
-        acc_tiles = {}
-        g_tiles = {}
-        tb_tiles = {}
-        o_tiles = {}
-
-        def XT(pair, g):
-            xt = ps_tr.tile([P, 2, 256], F32, name="xt", tag="tr")
+        def transpose_x(pair, g):
+            xt = ps_tr.tile([P, 2, 2 * P], F32, name="xt", tag="tr")
             for u in range(2):
                 for i in range(2):
                     words = x_raw[pair][:, i, :].bitcast(F32)
                     j = 2 * g + u
                     nc.tensor.transpose(xt[:, u, P * i : P * i + P], words[:, P * j : P * j + P], ident_f[:])
-            xt_tiles[(pair, g)] = xt
+            tiles["xt", pair, g] = xt
 
-        def XC(pair, g, eng):
-            xg = xg_pool.tile([P, 1024], BF16, name="xg", align_bytes=64)
+        def copy_x(pair, g, on_scalar):
+            xg = xg_pool.tile([P, PACK * 2 * P], BF16, name="xg", align_bytes=64)
             dst = xg[:].bitcast(F32).rearrange("p (c u) -> p c u", u=2)
-            src = xt_tiles[(pair, g)][:].rearrange("p u c -> p c u")
-            if eng == "S":
+            src = tiles["xt", pair, g][:].rearrange("p u c -> p c u")
+            if on_scalar:
                 nc.scalar.copy(out=dst, in_=src)
             else:
                 nc.vector.tensor_copy(out=dst, in_=src)
-            xg_tiles[(pair, g)] = xg
+            tiles["xg", pair, g] = xg
 
-        def XQ(pair, g):
-            cols = slice(256 * pair, 256 * pair + 256)
+        def quantise_x(pair, g):
+            cols = slice(2 * P * pair, 2 * P * pair + 2 * P)
             nc.vector.quantize_mx(
-                out=x_codes[:, g, cols].bitcast(FP8X4), scales=x_scales[:, g, cols], in_=xg_tiles[(pair, g)][:]
+                out=x_codes[:, g, cols].bitcast(FP8X4), scales=x_scales[:, g, cols], in_=tiles["xg", pair, g][:]
             )
 
-        def WR(nb, g, eng, c0, c1):
-            if (nb, g) not in wg_tiles:
-                wg_tiles[(nb, g)] = wg_pool.tile([P, BLOCK, 4], BF16, name="wg", align_bytes=64)
-            wg = wg_tiles[(nb, g)]
-            dst = wg[:, c0:c1, :].rearrange("p (c i) t -> p c t i", i=4)
-            src = w_raw[nb][:, 4 * g : 4 * g + 4, c0:c1].rearrange("p t (c i) -> p c t i", i=4)
-            if eng == "S":
-                nc.scalar.copy(out=dst, in_=src)
-            else:
-                nc.vector.tensor_copy(out=dst, in_=src)
+        def regroup_w(nb, g):
+            wg = wg_pool.tile([P, BLOCK, PACK], BF16, name="wg", align_bytes=64)
+            split = VECTOR_COLS if nb < SHARED_BLOCKS and g > 0 else BLOCK
+            for c0, c1 in ((0, split), (split, BLOCK)):
+                if c0 == c1:
+                    continue
+                dst = wg[:, c0:c1, :].rearrange("p (c i) t -> p c t i", i=4)
+                src = w_raw[nb][:, PACK * g : PACK * g + PACK, c0:c1].rearrange("p t (c i) -> p c t i", i=4)
+                if c0 == 0:
+                    nc.vector.tensor_copy(out=dst, in_=src)
+                else:
+                    nc.scalar.copy(out=dst, in_=src)
+            tiles["wg", nb, g] = wg
 
-        def WQ(nb, g):
+        def quantise_w(nb, g):
             cols = slice(BLOCK * nb, BLOCK * nb + BLOCK)
             nc.vector.quantize_mx(
                 out=w_codes[:, g, cols].bitcast(FP8X4),
                 scales=w_scales[:, g, cols],
-                in_=wg_tiles[(nb, g)][:].rearrange("p n t -> p (n t)"),
+                in_=tiles["wg", nb, g][:].rearrange("p n t -> p (n t)"),
             )
 
         def mx_pass(u, i, g):
             nb, h = divmod(u, 2)
             if g == 0:
-                acc_tiles[(u, i)] = ps_acc.tile([P, HALF], F32, name="acc", tag="acc")
-            nt = 4 * nb + i
-            n_cols = slice(P * nt, P * nt + P)
+                tiles["acc", u, i] = ps_acc.tile([P, HALF], F32, name="acc", tag="acc")
+            n_cols = slice(BLOCK * nb + P * i, BLOCK * nb + P * i + P)
             b_cols = slice(HALF * h, HALF * h + HALF)
             nc.tensor.matmul_mx(
-                out=acc_tiles[(u, i)][:],
+                out=tiles["acc", u, i][:],
                 lhsT=w_codes[:, g, n_cols].bitcast(FP8X4),
                 lhsT_scale=w_scales[:, g, n_cols],
                 rhs=x_codes[:, g, b_cols].bitcast(FP8X4),
@@ -191,365 +175,129 @@ def tile_modelnew_kernel(tc, x, weight, bn_gamma, bn_beta, bn_mean, bn_var, out)
                 stop=(g == PASSES - 1),
             )
 
-        def MX(u, i):
+        def multiply(u, i):
             for g in range(PASSES):
                 mx_pass(u, i, g)
 
-        def MXg(u, g):
-            for i in range(4):
-                mx_pass(u, i, g)
-
-        def GE(u, i):
-            nt = 4 * (u // 2) + i
+        def first_exit(u, i):
+            col = COL_TILES * (u // 2) + i
             g_t = g_pool.tile([P, HALF], F32, name="g_t")
             nc.scalar.activation(
-                out=g_t[:], in_=acc_tiles[(u, i)][:],
+                out=g_t[:],
+                in_=tiles["acc", u, i][:],
                 func=(ACT.Gelu_apprx_tanh if i % 2 == 0 else ACT.Relu),
-                bias=t_col[:, nt : nt + 1], scale=s_col[:, nt : nt + 1],
+                bias=t_col[:, col : col + 1],
+                scale=s_col[:, col : col + 1],
             )
-            g_tiles[(u, i)] = g_t
+            tiles["g", u, i] = g_t
 
-        def TB(u, i):
-            tb = ps_tr.tile([P, 4, P], F32, name="tb", tag="tr")
-            for tt in range(4):
-                nc.tensor.transpose(tb[:, tt, :], g_tiles[(u, i)][:, P * tt : P * tt + P], ident_f[:])
-            tb_tiles[(u, i)] = tb
+        def turn_back(u, i):
+            tb = ps_tr.tile([P, HALF_TILES, P], F32, name="tb", tag="tr")
+            for tt in range(HALF_TILES):
+                nc.tensor.transpose(tb[:, tt, :], tiles["g", u, i][:, P * tt : P * tt + P], ident_f[:])
+            tiles["tb", u, i] = tb
 
-        def RX(u, i):
-            if u not in o_tiles:
-                o_tiles[u] = o_pool.tile([P, 4, BLOCK], F32, name="o_sb")
-            dst = o_tiles[u][:, :, P * i : P * i + P]
+        def second_exit(u, i):
+            if i == 0:
+                tiles["o", u] = o_pool.tile([P, HALF_TILES, BLOCK], F32, name="o_sb")
+            dst = tiles["o", u][:, :, P * i : P * i + P]
             if i % 2 == 0:
-                nc.vector.tensor_scalar(dst, tb_tiles[(u, i)][:], 0.0, 0.0, op0=ALU.max, op1=ALU.add)
+                nc.vector.tensor_scalar(dst, tiles["tb", u, i][:], 0.0, 0.0, op0=ALU.max, op1=ALU.add)
             else:
-                nc.scalar.activation(out=dst, in_=tb_tiles[(u, i)][:], func=ACT.Gelu_apprx_tanh)
+                nc.scalar.activation(out=dst, in_=tiles["tb", u, i][:], func=ACT.Gelu_apprx_tanh)
 
-        def ST(u, i0, i1):
+        def finish(u, i):
+            turn_back(u, i)
+            second_exit(u, i)
+
+        def store(u, i0, i1):
             nb, h = divmod(u, 2)
             nc.sync.dma_start(
-                out=out_v[:, 4 * h : 4 * h + 4, BLOCK * nb + P * i0 : BLOCK * nb + P * i1],
-                in_=o_tiles[u][:, :, P * i0 : P * i1],
+                out=out_v[:, HALF_TILES * h : HALF_TILES * h + HALF_TILES, BLOCK * nb + P * i0 : BLOCK * nb + P * i1],
+                in_=tiles["o", u][:, :, P * i0 : P * i1],
             )
 
-        WARM()
-        XT(0, 0)
-        XT(0, 1)
-        XC(0, 0, "S")
-        XT(0, 2)
-        XC(0, 1, "S")
-        XQ(0, 0)
-        XT(0, 3)
-        XC(0, 2, "S")
-        XQ(0, 1)
-        PT()
-        XC(0, 3, "S")
-        XT(1, 0)
-        XQ(0, 2)
-        XT(1, 1)
-        XQ(0, 3)
-        XC(1, 0, "S")
-        PC()
-        XT(1, 2)
-        WR(0, 0, "V", 0, 512)
-        XC(1, 1, "S")
-        PW()
-        XT(1, 3)
-        XC(1, 2, "S")
-        XQ(1, 0)
-        XC(1, 3, "S")
-        WQ(0, 0)
-        WR(0, 1, "S", 192, 512)
-        XQ(1, 1)
-        WR(0, 1, "V", 0, 192)
-        mx_pass(0, 0, 0)
-        XQ(1, 2)
-        mx_pass(0, 1, 0)
-        WR(0, 2, "S", 192, 512)
-        mx_pass(0, 2, 0)
-        WQ(0, 1)
-        mx_pass(0, 3, 0)
-        XQ(1, 3)
-        WR(0, 2, "V", 0, 192)
-        mx_pass(0, 0, 1)
-        mx_pass(0, 1, 1)
-        WR(0, 3, "S", 192, 512)
-        WQ(0, 2)
-        mx_pass(0, 2, 1)
-        mx_pass(0, 3, 1)
-        WR(0, 3, "V", 0, 192)
-        mx_pass(0, 0, 2)
-        mx_pass(0, 1, 2)
-        WQ(0, 3)
-        mx_pass(0, 2, 2)
-        mx_pass(0, 3, 2)
-        STt()
-        XT(2, 0)
-        XT(2, 1)
-        XC(2, 0, "V")
-        XT(2, 2)
-        XC(2, 1, "S")
-        XT(2, 3)
-        XQ(2, 0)
-        XC(2, 2, "V")
-        XC(2, 3, "S")
-        mx_pass(0, 0, 3)
-        mx_pass(0, 1, 3)
-        XQ(2, 1)
-        GE(0, 0)
-        mx_pass(0, 2, 3)
-        XQ(2, 2)
-        mx_pass(0, 3, 3)
-        XQ(2, 3)
-        GE(0, 1)
-        XT(3, 0)
-        XT(3, 1)
-        XC(3, 0, "V")
-        XT(3, 2)
-        XC(3, 1, "S")
-        XT(3, 3)
-        XQ(3, 0)
-        TB(0, 0)
-        XC(3, 2, "V")
-        XC(3, 3, "S")
-        TB(0, 1)
-        XQ(3, 1)
-        GE(0, 2)
-        mx_pass(1, 0, 0)
-        XQ(3, 2)
-        XQ(3, 3)
-        mx_pass(1, 0, 1)
-        GE(0, 3)
-        WR(1, 0, "V", 0, 512)
-        mx_pass(1, 0, 2)
-        mx_pass(1, 0, 3)
-        WR(1, 1, "S", 0, 512)
-        mx_pass(1, 1, 0)
-        mx_pass(1, 1, 1)
-        mx_pass(1, 1, 2)
-        WQ(1, 0)
-        mx_pass(1, 1, 3)
-        mx_pass(1, 2, 0)
-        WR(1, 2, "V", 0, 512)
-        mx_pass(1, 2, 1)
-        mx_pass(1, 2, 2)
-        GE(1, 0)
-        mx_pass(1, 2, 3)
-        mx_pass(1, 3, 0)
-        WQ(1, 1)
-        mx_pass(1, 3, 1)
-        GE(1, 1)
-        mx_pass(1, 3, 2)
-        WR(1, 3, "V", 0, 512)
-        mx_pass(1, 3, 3)
-        GE(1, 2)
-        TB(0, 2)
-        GE(1, 3)
-        TB(0, 3)
-        WQ(1, 2)
-        mx_pass(2, 0, 0)
-        RX(0, 1)
-        mx_pass(2, 0, 1)
-        WQ(1, 3)
-        mx_pass(2, 0, 2)
-        RX(0, 3)
-        RX(0, 0)
-        mx_pass(2, 0, 3)
-        RX(0, 2)
-        mx_pass(2, 1, 0)
-        GE(2, 0)
-        mx_pass(2, 1, 1)
-        mx_pass(2, 1, 2)
-        WR(2, 0, "V", 0, 512)
-        mx_pass(2, 1, 3)
-        mx_pass(2, 2, 0)
-        GE(2, 1)
-        mx_pass(2, 2, 1)
-        ST(0, 0, 4)
-        mx_pass(2, 2, 2)
-        WR(2, 1, "V", 0, 512)
-        mx_pass(2, 2, 3)
-        mx_pass(2, 3, 0)
-        GE(2, 2)
-        mx_pass(2, 3, 1)
-        mx_pass(2, 3, 2)
-        WQ(2, 0)
-        mx_pass(2, 3, 3)
-        WQ(2, 1)
-        GE(2, 3)
-        TB(1, 0)
-        TB(1, 1)
-        RX(1, 0)
-        TB(1, 2)
-        RX(1, 1)
-        TB(1, 3)
-        RX(1, 2)
-        RX(1, 3)
-        mx_pass(3, 0, 0)
-        mx_pass(3, 0, 1)
-        WR(2, 2, "V", 0, 512)
-        mx_pass(3, 0, 2)
-        ST(1, 0, 4)
-        mx_pass(3, 0, 3)
-        mx_pass(3, 1, 0)
-        GE(3, 0)
-        mx_pass(3, 1, 1)
-        WR(2, 3, "V", 0, 512)
-        mx_pass(3, 1, 2)
-        mx_pass(3, 1, 3)
-        mx_pass(3, 2, 0)
-        GE(3, 1)
-        mx_pass(3, 2, 1)
-        WQ(2, 2)
-        mx_pass(3, 2, 2)
-        mx_pass(3, 2, 3)
-        WQ(2, 3)
-        mx_pass(3, 3, 0)
-        GE(3, 2)
-        mx_pass(3, 3, 1)
-        mx_pass(3, 3, 2)
-        mx_pass(3, 3, 3)
-        GE(3, 3)
-        TB(2, 0)
-        TB(2, 1)
-        RX(2, 0)
-        TB(2, 2)
-        RX(2, 1)
-        TB(2, 3)
-        RX(2, 2)
-        RX(2, 3)
-        mx_pass(4, 0, 0)
-        WR(3, 0, "V", 0, 512)
-        mx_pass(4, 0, 1)
-        mx_pass(4, 0, 2)
-        ST(2, 0, 4)
-        mx_pass(4, 0, 3)
-        mx_pass(4, 1, 0)
-        GE(4, 0)
-        WR(3, 1, "V", 0, 512)
-        mx_pass(4, 1, 1)
-        mx_pass(4, 1, 2)
-        mx_pass(4, 1, 3)
-        mx_pass(4, 2, 0)
-        GE(4, 1)
-        WQ(3, 0)
-        mx_pass(4, 2, 1)
-        mx_pass(4, 2, 2)
-        WQ(3, 1)
-        mx_pass(4, 2, 3)
-        mx_pass(4, 3, 0)
-        GE(4, 2)
-        mx_pass(4, 3, 1)
-        mx_pass(4, 3, 2)
-        mx_pass(4, 3, 3)
-        GE(4, 3)
-        TB(3, 0)
-        TB(3, 1)
-        RX(3, 0)
-        TB(3, 2)
-        RX(3, 1)
-        TB(3, 3)
-        RX(3, 2)
-        RX(3, 3)
-        mx_pass(5, 0, 0)
-        WR(3, 2, "V", 0, 512)
-        mx_pass(5, 0, 1)
-        mx_pass(5, 0, 2)
-        ST(3, 0, 4)
-        mx_pass(5, 0, 3)
-        mx_pass(5, 1, 0)
-        GE(5, 0)
-        WR(3, 3, "V", 0, 512)
-        mx_pass(5, 1, 1)
-        mx_pass(5, 1, 2)
-        mx_pass(5, 1, 3)
-        mx_pass(5, 2, 0)
-        GE(5, 1)
-        WQ(3, 2)
-        mx_pass(5, 2, 1)
-        mx_pass(5, 2, 2)
-        WQ(3, 3)
-        mx_pass(5, 2, 3)
-        mx_pass(5, 3, 0)
-        GE(5, 2)
-        mx_pass(5, 3, 1)
-        mx_pass(5, 3, 2)
-        mx_pass(5, 3, 3)
-        GE(5, 3)
-        TB(4, 0)
-        TB(4, 1)
-        RX(4, 0)
-        TB(4, 2)
-        RX(4, 1)
-        TB(4, 3)
-        RX(4, 2)
-        RX(4, 3)
-        mx_pass(6, 0, 0)
-        mx_pass(6, 0, 1)
-        mx_pass(6, 0, 2)
-        ST(4, 0, 4)
-        mx_pass(6, 0, 3)
-        mx_pass(6, 1, 0)
-        GE(6, 0)
-        mx_pass(6, 1, 1)
-        mx_pass(6, 1, 2)
-        mx_pass(6, 1, 3)
-        mx_pass(6, 2, 0)
-        GE(6, 1)
-        mx_pass(6, 2, 1)
-        mx_pass(6, 2, 2)
-        mx_pass(6, 2, 3)
-        mx_pass(6, 3, 0)
-        GE(6, 2)
-        mx_pass(6, 3, 1)
-        mx_pass(6, 3, 2)
-        mx_pass(6, 3, 3)
-        GE(6, 3)
-        TB(5, 0)
-        TB(5, 1)
-        RX(5, 0)
-        TB(5, 2)
-        RX(5, 1)
-        TB(5, 3)
-        RX(5, 2)
-        RX(5, 3)
-        mx_pass(7, 0, 0)
-        mx_pass(7, 0, 1)
-        mx_pass(7, 0, 2)
-        ST(5, 0, 4)
-        mx_pass(7, 0, 3)
-        GE(7, 0)
-        TB(6, 0)
-        TB(6, 1)
-        RX(6, 0)
-        TB(6, 2)
-        RX(6, 1)
-        TB(6, 3)
-        RX(6, 2)
-        RX(6, 3)
-        mx_pass(7, 1, 0)
-        mx_pass(7, 1, 1)
-        mx_pass(7, 1, 2)
-        ST(6, 0, 4)
-        mx_pass(7, 1, 3)
-        mx_pass(7, 2, 0)
-        GE(7, 1)
-        mx_pass(7, 2, 1)
-        mx_pass(7, 2, 2)
-        mx_pass(7, 2, 3)
-        GE(7, 2)
-        TB(7, 0)
-        TB(7, 1)
-        RX(7, 0)
-        RX(7, 1)
-        mx_pass(7, 3, 0)
-        mx_pass(7, 3, 1)
-        mx_pass(7, 3, 2)
-        ST(7, 0, 2)
-        mx_pass(7, 3, 3)
-        GE(7, 3)
-        TB(7, 2)
-        RX(7, 2)
-        TB(7, 3)
-        RX(7, 3)
-        ST(7, 2, 3)
-        ST(7, 3, 4)
+        load_gelu_table()
+        for g in range(PASSES):
+            transpose_x(0, g)
+        transpose_params()
+        for g in range(PASSES):
+            copy_x(0, g, True)
+            quantise_x(0, g)
+        inverse_std()
+        for g in range(PASSES):
+            transpose_x(1, g)
+        for g in range(PASSES):
+            copy_x(1, g, True)
+
+        for g in range(PASSES):
+            regroup_w(0, g)
+            quantise_x(1, g)
+            quantise_w(0, g)
+            if g == PASSES - 1:
+                scale_and_shift()
+                for gg in range(PASSES):
+                    transpose_x(2, gg)
+            for i in range(COL_TILES):
+                mx_pass(0, i, g)
+
+        for pair in (2, 3):
+            if pair == 3:
+                for g in range(PASSES):
+                    transpose_x(3, g)
+                turn_back(0, 0)
+                turn_back(0, 1)
+            for g in range(PASSES):
+                copy_x(pair, g, g % 2 == 1)
+            for g in range(PASSES):
+                quantise_x(pair, g)
+            first_exit(0, 2 * pair - 4)
+            first_exit(0, 2 * pair - 3)
+
+        for i in range(COL_TILES):
+            multiply(1, i)
+        turn_back(0, 2)
+        turn_back(0, 3)
+        regroup_w(1, 0)
+        for g in range(1, PASSES):
+            regroup_w(1, g)
+            quantise_w(1, g - 1)
+        quantise_w(1, PASSES - 1)
+        for i in range(COL_TILES):
+            first_exit(1, i)
+        for i in range(COL_TILES):
+            second_exit(0, i)
+        store(0, 0, COL_TILES)
+
+        for u in range(2, LAST):
+            nb, h = divmod(u, 2)
+            for i in range(COL_TILES):
+                multiply(u, i)
+                first_exit(u, i)
+            if nb + 1 < N_BLOCKS:
+                regroup_w(nb + 1, 2 * h)
+                regroup_w(nb + 1, 2 * h + 1)
+                quantise_w(nb + 1, 2 * h)
+                quantise_w(nb + 1, 2 * h + 1)
+            for i in range(COL_TILES):
+                finish(u - 1, i)
+            store(u - 1, 0, COL_TILES)
+
+        multiply(LAST, 0)
+        first_exit(LAST, 0)
+        for i in range(COL_TILES):
+            finish(LAST - 1, i)
+        store(LAST - 1, 0, COL_TILES)
+        multiply(LAST, 1)
+        first_exit(LAST, 1)
+        multiply(LAST, 2)
+        first_exit(LAST, 2)
+        finish(LAST, 0)
+        finish(LAST, 1)
+        store(LAST, 0, 2)
+        multiply(LAST, 3)
+        first_exit(LAST, 3)
+        finish(LAST, 2)
+        store(LAST, 2, 3)
+        finish(LAST, 3)
+        store(LAST, 3, 4)

@@ -29,6 +29,7 @@ UNITS = 2 * N_BLOCKS
 LAST = UNITS - 1
 SHARED_BLOCKS = 2
 VECTOR_COLS = BLOCK // 2
+VEC_COLS = N // P
 
 
 def tile_modelnew_kernel(tc, x, weight, bn_gamma, bn_beta, bn_mean, bn_var, out):
@@ -40,8 +41,8 @@ def tile_modelnew_kernel(tc, x, weight, bn_gamma, bn_beta, bn_mean, bn_var, out)
         const = ctx.enter_context(tc.tile_pool(name="const", bufs=1))
         keep = ctx.enter_context(tc.tile_pool(name="keep", bufs=1))
         wg_pool = ctx.enter_context(tc.tile_pool(name="wg_pool", bufs=3))
-        xg_pool = ctx.enter_context(tc.tile_pool(name="xg_pool", bufs=2 * PASSES))
-        g_pool = ctx.enter_context(tc.tile_pool(name="g_pool", bufs=2 * COL_TILES))
+        xg_pool = ctx.enter_context(tc.tile_pool(name="xg_pool", bufs=PASSES + 2))
+        y_pool = ctx.enter_context(tc.tile_pool(name="y_pool", bufs=3 * COL_TILES))
         o_pool = ctx.enter_context(tc.tile_pool(name="o_pool", bufs=3))
         ps_acc = ctx.enter_context(tc.psum_pool(name="ps_acc", bufs=4))
         ps_tr = ctx.enter_context(tc.psum_pool(name="ps_tr", bufs=4))
@@ -59,7 +60,7 @@ def tile_modelnew_kernel(tc, x, weight, bn_gamma, bn_beta, bn_mean, bn_var, out)
 
         def load_w(nb):
             for j in range(2 * PASSES):
-                rows = weight[256 * j : 256 * j + 256, BLOCK * nb : BLOCK * nb + BLOCK]
+                rows = weight[2 * P * j : 2 * P * j + 2 * P, BLOCK * nb : BLOCK * nb + BLOCK]
                 nc.sync.dma_start(
                     out=w_raw[nb][:, 2 * j : 2 * j + 2, :],
                     in_=rows.rearrange("(q e) n -> q e n", e=2),
@@ -68,7 +69,9 @@ def tile_modelnew_kernel(tc, x, weight, bn_gamma, bn_beta, bn_mean, bn_var, out)
         p_rows = const.tile([P, P], BF16, name="p_rows")
         nc.vector.memset(p_rows[:], 0.0)
         for v, vec in enumerate((bn_gamma, bn_beta, bn_mean, bn_var)):
-            nc.scalar.dma_start(out=p_rows[16 * v : 16 * v + 16, :], in_=vec.rearrange("(r c) -> r c", c=P))
+            nc.scalar.dma_start(
+                out=p_rows[VEC_COLS * v : VEC_COLS * v + VEC_COLS, :], in_=vec.rearrange("(r c) -> r c", c=P)
+            )
         load_x(0)
         load_x(1)
         load_w(0)
@@ -81,15 +84,18 @@ def tile_modelnew_kernel(tc, x, weight, bn_gamma, bn_beta, bn_mean, bn_var, out)
         make_identity(nc, ident_f[:])
         ident_b = const.tile([P, P], BF16, name="ident_b")
         make_identity(nc, ident_b[:])
-        minus_half = const.tile([P, 16], F32, name="minus_half")
+        minus_half = const.tile([P, VEC_COLS], F32, name="minus_half")
         nc.gpsimd.memset(minus_half[:], -0.5)
 
-        p_cols = const.tile([P, 48], F32, name="p_cols")
-        var_eps = const.tile([P, 16], F32, name="var_eps")
-        rstd = const.tile([P, 16], F32, name="rstd")
-        s_col = const.tile([P, 16], F32, name="s_col")
-        mean_s = const.tile([P, 16], F32, name="mean_s")
-        t_col = const.tile([P, 16], F32, name="t_col")
+        p_cols = const.tile([P, 3 * VEC_COLS], F32, name="p_cols")
+        gamma_cols = p_cols[:, 0:VEC_COLS]
+        beta_cols = p_cols[:, VEC_COLS : 2 * VEC_COLS]
+        mean_cols = p_cols[:, 2 * VEC_COLS : 3 * VEC_COLS]
+        var_eps = const.tile([P, VEC_COLS], F32, name="var_eps")
+        rstd = const.tile([P, VEC_COLS], F32, name="rstd")
+        scale_cols = const.tile([P, VEC_COLS], F32, name="scale_cols")
+        mean_scale = const.tile([P, VEC_COLS], F32, name="mean_scale")
+        shift_cols = const.tile([P, VEC_COLS], F32, name="shift_cols")
         warm_in = const.tile([P, 1], F32, name="warm_in")
         warm_out = const.tile([P, 1], F32, name="warm_out")
         nc.vector.memset(warm_in[:], 0.0)
@@ -103,28 +109,28 @@ def tile_modelnew_kernel(tc, x, weight, bn_gamma, bn_beta, bn_mean, bn_var, out)
             nc.tensor.transpose(tiles["params"][:], p_rows[:], ident_b[:])
 
         def inverse_std():
-            nc.vector.tensor_copy(out=p_cols[:], in_=tiles["params"][:, 0:48])
-            nc.vector.tensor_scalar_add(var_eps[:], tiles["params"][:, 48:64], EPS)
+            nc.vector.tensor_copy(out=p_cols[:], in_=tiles["params"][:, 0 : 3 * VEC_COLS])
+            nc.vector.tensor_scalar_add(var_eps[:], tiles["params"][:, 3 * VEC_COLS : 4 * VEC_COLS], EPS)
             nc.gpsimd.tensor_tensor(out=rstd[:], in0=var_eps[:], in1=minus_half[:], op=ALU.pow)
 
         def scale_and_shift():
-            nc.vector.tensor_mul(s_col[:], p_cols[:, 0:16], rstd[:])
-            nc.vector.tensor_mul(mean_s[:], p_cols[:, 32:48], s_col[:])
-            nc.vector.tensor_sub(t_col[:], p_cols[:, 16:32], mean_s[:])
+            nc.vector.tensor_mul(scale_cols[:], gamma_cols, rstd[:])
+            nc.vector.tensor_mul(mean_scale[:], mean_cols, scale_cols[:])
+            nc.vector.tensor_sub(shift_cols[:], beta_cols, mean_scale[:])
 
         def transpose_x(pair, g):
             xt = ps_tr.tile([P, 2, 2 * P], F32, name="xt", tag="tr")
-            for u in range(2):
-                for i in range(2):
-                    words = x_raw[pair][:, i, :].bitcast(F32)
-                    j = 2 * g + u
-                    nc.tensor.transpose(xt[:, u, P * i : P * i + P], words[:, P * j : P * j + P], ident_f[:])
+            for a in range(2):
+                for r in range(2):
+                    words = x_raw[pair][:, r, :].bitcast(F32)
+                    j = 2 * g + a
+                    nc.tensor.transpose(xt[:, a, P * r : P * r + P], words[:, P * j : P * j + P], ident_f[:])
             tiles["xt", pair, g] = xt
 
         def copy_x(pair, g, on_scalar):
             xg = xg_pool.tile([P, PACK * 2 * P], BF16, name="xg", align_bytes=64)
-            dst = xg[:].bitcast(F32).rearrange("p (c u) -> p c u", u=2)
-            src = tiles["xt", pair, g][:].rearrange("p u c -> p c u")
+            dst = xg[:].bitcast(F32).rearrange("p (c a) -> p c a", a=2)
+            src = tiles["xt", pair, g][:].rearrange("p a c -> p c a")
             if on_scalar:
                 nc.scalar.copy(out=dst, in_=src)
             else:
@@ -143,8 +149,8 @@ def tile_modelnew_kernel(tc, x, weight, bn_gamma, bn_beta, bn_mean, bn_var, out)
             for c0, c1 in ((0, split), (split, BLOCK)):
                 if c0 == c1:
                     continue
-                dst = wg[:, c0:c1, :].rearrange("p (c i) t -> p c t i", i=4)
-                src = w_raw[nb][:, PACK * g : PACK * g + PACK, c0:c1].rearrange("p t (c i) -> p c t i", i=4)
+                dst = wg[:, c0:c1, :].rearrange("p (c r) v -> p c v r", r=4)
+                src = w_raw[nb][:, PACK * g : PACK * g + PACK, c0:c1].rearrange("p v (c r) -> p c v r", r=4)
                 if c0 == 0:
                     nc.vector.tensor_copy(out=dst, in_=src)
                 else:
@@ -156,7 +162,7 @@ def tile_modelnew_kernel(tc, x, weight, bn_gamma, bn_beta, bn_mean, bn_var, out)
             nc.vector.quantize_mx(
                 out=w_codes[:, g, cols].bitcast(FP8X4),
                 scales=w_scales[:, g, cols],
-                in_=tiles["wg", nb, g][:].rearrange("p n t -> p (n t)"),
+                in_=tiles["wg", nb, g][:].rearrange("p n v -> p (n v)"),
             )
 
         def mx_pass(u, i, g):
@@ -181,20 +187,20 @@ def tile_modelnew_kernel(tc, x, weight, bn_gamma, bn_beta, bn_mean, bn_var, out)
 
         def first_exit(u, i):
             col = COL_TILES * (u // 2) + i
-            g_t = g_pool.tile([P, HALF], F32, name="g_t")
+            y_t = y_pool.tile([P, HALF], F32, name="y_t")
             nc.scalar.activation(
-                out=g_t[:],
+                out=y_t[:],
                 in_=tiles["acc", u, i][:],
                 func=(ACT.Gelu_apprx_tanh if i % 2 == 0 else ACT.Relu),
-                bias=t_col[:, col : col + 1],
-                scale=s_col[:, col : col + 1],
+                bias=shift_cols[:, col : col + 1],
+                scale=scale_cols[:, col : col + 1],
             )
-            tiles["g", u, i] = g_t
+            tiles["y", u, i] = y_t
 
         def turn_back(u, i):
             tb = ps_tr.tile([P, HALF_TILES, P], F32, name="tb", tag="tr")
             for tt in range(HALF_TILES):
-                nc.tensor.transpose(tb[:, tt, :], tiles["g", u, i][:, P * tt : P * tt + P], ident_f[:])
+                nc.tensor.transpose(tb[:, tt, :], tiles["y", u, i][:, P * tt : P * tt + P], ident_f[:])
             tiles["tb", u, i] = tb
 
         def second_exit(u, i):
@@ -251,8 +257,8 @@ def tile_modelnew_kernel(tc, x, weight, bn_gamma, bn_beta, bn_mean, bn_var, out)
                 copy_x(pair, g, g % 2 == 1)
             for g in range(PASSES):
                 quantise_x(pair, g)
-            first_exit(0, 2 * pair - 4)
-            first_exit(0, 2 * pair - 3)
+            first_exit(0, 2 * (pair - 2))
+            first_exit(0, 2 * (pair - 2) + 1)
 
         for i in range(COL_TILES):
             multiply(1, i)
@@ -269,25 +275,31 @@ def tile_modelnew_kernel(tc, x, weight, bn_gamma, bn_beta, bn_mean, bn_var, out)
             second_exit(0, i)
         store(0, 0, COL_TILES)
 
-        for u in range(2, LAST):
-            nb, h = divmod(u, 2)
+        def whole_unit(u):
             for i in range(COL_TILES):
                 multiply(u, i)
                 first_exit(u, i)
-            if nb + 1 < N_BLOCKS:
+
+        def finish_unit(u):
+            for i in range(COL_TILES):
+                finish(u, i)
+            store(u, 0, COL_TILES)
+
+        for nb in range(1, N_BLOCKS - 1):
+            for h in range(2):
+                whole_unit(2 * nb + h)
                 regroup_w(nb + 1, 2 * h)
                 regroup_w(nb + 1, 2 * h + 1)
                 quantise_w(nb + 1, 2 * h)
                 quantise_w(nb + 1, 2 * h + 1)
-            for i in range(COL_TILES):
-                finish(u - 1, i)
-            store(u - 1, 0, COL_TILES)
+            finish_unit(2 * nb - 1)
+            finish_unit(2 * nb)
 
+        whole_unit(LAST - 1)
         multiply(LAST, 0)
         first_exit(LAST, 0)
-        for i in range(COL_TILES):
-            finish(LAST - 1, i)
-        store(LAST - 1, 0, COL_TILES)
+        finish_unit(LAST - 2)
+        finish_unit(LAST - 1)
         multiply(LAST, 1)
         first_exit(LAST, 1)
         multiply(LAST, 2)
@@ -300,4 +312,4 @@ def tile_modelnew_kernel(tc, x, weight, bn_gamma, bn_beta, bn_mean, bn_var, out)
         finish(LAST, 2)
         store(LAST, 2, 3)
         finish(LAST, 3)
-        store(LAST, 3, 4)
+        store(LAST, 3, COL_TILES)

from contextlib import ExitStack

import concourse.mybir as mybir
from concourse.masks import make_identity

FP8X4 = mybir.dt.float8_e4m3fn_x4
BF16 = mybir.dt.bfloat16
F32 = mybir.dt.float32
U32 = mybir.dt.uint32
U8 = mybir.dt.uint8
ACT = mybir.ActivationFunctionType
ALU = mybir.AluOpType

B, K, N = 1024, 2048, 2048
EPS = 1e-5
FLOPS = 2 * B * K * N

P = 128
PACK = 4
PASSES = K // (P * PACK)
ROW_TILES = B // P
PAIRS = ROW_TILES // 2
HALF_TILES = 4
HALF = HALF_TILES * P
COL_TILES = 4
BLOCK = COL_TILES * P
N_BLOCKS = N // BLOCK
UNITS = 2 * N_BLOCKS
LAST = UNITS - 1
SHARED_BLOCKS = 2
VECTOR_COLS = BLOCK // 2
VEC_COLS = N // P


def tile_modelnew_kernel(tc, x, weight, bn_gamma, bn_beta, bn_mean, bn_var, out):
    nc = tc.nc
    x_v = x.rearrange("(p t) k -> p t k", t=ROW_TILES)
    out_v = out.rearrange("(p t) n -> p t n", t=ROW_TILES)

    with ExitStack() as ctx:
        const = ctx.enter_context(tc.tile_pool(name="const", bufs=1))
        keep = ctx.enter_context(tc.tile_pool(name="keep", bufs=1))
        wg_pool = ctx.enter_context(tc.tile_pool(name="wg_pool", bufs=3))
        xg_pool = ctx.enter_context(tc.tile_pool(name="xg_pool", bufs=PASSES + 2))
        y_pool = ctx.enter_context(tc.tile_pool(name="y_pool", bufs=3 * COL_TILES))
        o_pool = ctx.enter_context(tc.tile_pool(name="o_pool", bufs=3))
        ps_acc = ctx.enter_context(tc.psum_pool(name="ps_acc", bufs=4))
        ps_tr = ctx.enter_context(tc.psum_pool(name="ps_tr", bufs=4))
        ctx.enter_context(tc.manual_schedule())

        x_raw = [keep.tile([P, 2, K], BF16, name="x_raw%d" % pair) for pair in range(PAIRS)]
        w_raw = [keep.tile([P, PACK * PASSES, BLOCK], BF16, name="w_raw%d" % nb) for nb in range(N_BLOCKS)]
        w_codes = keep.tile([P, PASSES, N], U32, name="w_codes", align_bytes=64)
        w_scales = keep.tile([P, PASSES, N], U8, name="w_scales", align_bytes=64)
        x_codes = keep.tile([P, PASSES, B], U32, name="x_codes", align_bytes=64)
        x_scales = keep.tile([P, PASSES, B], U8, name="x_scales", align_bytes=64)

        def load_x(pair):
            nc.sync.dma_start(out=x_raw[pair][:], in_=x_v[:, 2 * pair : 2 * pair + 2, :])

        def load_w(nb):
            for j in range(2 * PASSES):
                rows = weight[2 * P * j : 2 * P * j + 2 * P, BLOCK * nb : BLOCK * nb + BLOCK]
                nc.sync.dma_start(
                    out=w_raw[nb][:, 2 * j : 2 * j + 2, :],
                    in_=rows.rearrange("(q e) n -> q e n", e=2),
                )

        p_rows = const.tile([P, P], BF16, name="p_rows")
        nc.vector.memset(p_rows[:], 0.0)
        for v, vec in enumerate((bn_gamma, bn_beta, bn_mean, bn_var)):
            nc.scalar.dma_start(
                out=p_rows[VEC_COLS * v : VEC_COLS * v + VEC_COLS, :], in_=vec.rearrange("(r c) -> r c", c=P)
            )
        load_x(0)
        load_x(1)
        load_w(0)
        load_x(2)
        load_x(3)
        for nb in range(1, N_BLOCKS):
            load_w(nb)

        ident_f = const.tile([P, P], F32, name="ident_f")
        make_identity(nc, ident_f[:])
        ident_b = const.tile([P, P], BF16, name="ident_b")
        make_identity(nc, ident_b[:])
        minus_half = const.tile([P, VEC_COLS], F32, name="minus_half")
        nc.gpsimd.memset(minus_half[:], -0.5)

        p_cols = const.tile([P, 3 * VEC_COLS], F32, name="p_cols")
        gamma_cols = p_cols[:, 0:VEC_COLS]
        beta_cols = p_cols[:, VEC_COLS : 2 * VEC_COLS]
        mean_cols = p_cols[:, 2 * VEC_COLS : 3 * VEC_COLS]
        var_eps = const.tile([P, VEC_COLS], F32, name="var_eps")
        rstd = const.tile([P, VEC_COLS], F32, name="rstd")
        scale_cols = const.tile([P, VEC_COLS], F32, name="scale_cols")
        mean_scale = const.tile([P, VEC_COLS], F32, name="mean_scale")
        shift_cols = const.tile([P, VEC_COLS], F32, name="shift_cols")
        warm_in = const.tile([P, 1], F32, name="warm_in")
        warm_out = const.tile([P, 1], F32, name="warm_out")
        nc.vector.memset(warm_in[:], 0.0)
        tiles = {}

        def load_gelu_table():
            nc.scalar.activation(out=warm_out[:], in_=warm_in[:], func=ACT.Gelu_apprx_tanh)

        def transpose_params():
            tiles["params"] = ps_acc.tile([P, P], BF16, name="params", tag="acc")
            nc.tensor.transpose(tiles["params"][:], p_rows[:], ident_b[:])

        def inverse_std():
            nc.vector.tensor_copy(out=p_cols[:], in_=tiles["params"][:, 0 : 3 * VEC_COLS])
            nc.vector.tensor_scalar_add(var_eps[:], tiles["params"][:, 3 * VEC_COLS : 4 * VEC_COLS], EPS)
            nc.gpsimd.tensor_tensor(out=rstd[:], in0=var_eps[:], in1=minus_half[:], op=ALU.pow)

        def scale_and_shift():
            nc.vector.tensor_mul(scale_cols[:], gamma_cols, rstd[:])
            nc.vector.tensor_mul(mean_scale[:], mean_cols, scale_cols[:])
            nc.vector.tensor_sub(shift_cols[:], beta_cols, mean_scale[:])

        def transpose_x(pair, g):
            xt = ps_tr.tile([P, 2, 2 * P], F32, name="xt", tag="tr")
            for a in range(2):
                for r in range(2):
                    words = x_raw[pair][:, r, :].bitcast(F32)
                    j = 2 * g + a
                    nc.tensor.transpose(xt[:, a, P * r : P * r + P], words[:, P * j : P * j + P], ident_f[:])
            tiles["xt", pair, g] = xt

        def copy_x(pair, g, on_scalar):
            xg = xg_pool.tile([P, PACK * 2 * P], BF16, name="xg", align_bytes=64)
            dst = xg[:].bitcast(F32).rearrange("p (c a) -> p c a", a=2)
            src = tiles["xt", pair, g][:].rearrange("p a c -> p c a")
            if on_scalar:
                nc.scalar.copy(out=dst, in_=src)
            else:
                nc.vector.tensor_copy(out=dst, in_=src)
            tiles["xg", pair, g] = xg

        def quantise_x(pair, g):
            cols = slice(2 * P * pair, 2 * P * pair + 2 * P)
            nc.vector.quantize_mx(
                out=x_codes[:, g, cols].bitcast(FP8X4), scales=x_scales[:, g, cols], in_=tiles["xg", pair, g][:]
            )

        def regroup_w(nb, g):
            wg = wg_pool.tile([P, BLOCK, PACK], BF16, name="wg", align_bytes=64)
            split = VECTOR_COLS if nb < SHARED_BLOCKS and g > 0 else BLOCK
            for c0, c1 in ((0, split), (split, BLOCK)):
                if c0 == c1:
                    continue
                dst = wg[:, c0:c1, :].rearrange("p (c r) v -> p c v r", r=4)
                src = w_raw[nb][:, PACK * g : PACK * g + PACK, c0:c1].rearrange("p v (c r) -> p c v r", r=4)
                if c0 == 0:
                    nc.vector.tensor_copy(out=dst, in_=src)
                else:
                    nc.scalar.copy(out=dst, in_=src)
            tiles["wg", nb, g] = wg

        def quantise_w(nb, g):
            cols = slice(BLOCK * nb, BLOCK * nb + BLOCK)
            nc.vector.quantize_mx(
                out=w_codes[:, g, cols].bitcast(FP8X4),
                scales=w_scales[:, g, cols],
                in_=tiles["wg", nb, g][:].rearrange("p n v -> p (n v)"),
            )

        def mx_pass(u, i, g):
            nb, h = divmod(u, 2)
            if g == 0:
                tiles["acc", u, i] = ps_acc.tile([P, HALF], F32, name="acc", tag="acc")
            n_cols = slice(BLOCK * nb + P * i, BLOCK * nb + P * i + P)
            b_cols = slice(HALF * h, HALF * h + HALF)
            nc.tensor.matmul_mx(
                out=tiles["acc", u, i][:],
                lhsT=w_codes[:, g, n_cols].bitcast(FP8X4),
                lhsT_scale=w_scales[:, g, n_cols],
                rhs=x_codes[:, g, b_cols].bitcast(FP8X4),
                rhs_scale=x_scales[:, g, b_cols],
                start=(g == 0),
                stop=(g == PASSES - 1),
            )

        def multiply(u, i):
            for g in range(PASSES):
                mx_pass(u, i, g)

        def first_exit(u, i):
            col = COL_TILES * (u // 2) + i
            y_t = y_pool.tile([P, HALF], F32, name="y_t")
            nc.scalar.activation(
                out=y_t[:],
                in_=tiles["acc", u, i][:],
                func=(ACT.Gelu_apprx_tanh if i % 2 == 0 else ACT.Relu),
                bias=shift_cols[:, col : col + 1],
                scale=scale_cols[:, col : col + 1],
            )
            tiles["y", u, i] = y_t

        def turn_back(u, i):
            tb = ps_tr.tile([P, HALF_TILES, P], F32, name="tb", tag="tr")
            for tt in range(HALF_TILES):
                nc.tensor.transpose(tb[:, tt, :], tiles["y", u, i][:, P * tt : P * tt + P], ident_f[:])
            tiles["tb", u, i] = tb

        def second_exit(u, i):
            if i == 0:
                tiles["o", u] = o_pool.tile([P, HALF_TILES, BLOCK], F32, name="o_sb")
            dst = tiles["o", u][:, :, P * i : P * i + P]
            if i % 2 == 0:
                nc.vector.tensor_scalar(dst, tiles["tb", u, i][:], 0.0, 0.0, op0=ALU.max, op1=ALU.add)
            else:
                nc.scalar.activation(out=dst, in_=tiles["tb", u, i][:], func=ACT.Gelu_apprx_tanh)

        def finish(u, i):
            turn_back(u, i)
            second_exit(u, i)

        def store(u, i0, i1):
            nb, h = divmod(u, 2)
            nc.sync.dma_start(
                out=out_v[:, HALF_TILES * h : HALF_TILES * h + HALF_TILES, BLOCK * nb + P * i0 : BLOCK * nb + P * i1],
                in_=tiles["o", u][:, :, P * i0 : P * i1],
            )

        load_gelu_table()
        for g in range(PASSES):
            transpose_x(0, g)
        transpose_params()
        for g in range(PASSES):
            copy_x(0, g, True)
            quantise_x(0, g)
        inverse_std()
        for g in range(PASSES):
            transpose_x(1, g)
        for g in range(PASSES):
            copy_x(1, g, True)

        for g in range(PASSES):
            regroup_w(0, g)
            quantise_x(1, g)
            quantise_w(0, g)
            if g == PASSES - 1:
                scale_and_shift()
                for gg in range(PASSES):
                    transpose_x(2, gg)
            for i in range(COL_TILES):
                mx_pass(0, i, g)

        for pair in (2, 3):
            if pair == 3:
                for g in range(PASSES):
                    transpose_x(3, g)
                turn_back(0, 0)
                turn_back(0, 1)
            for g in range(PASSES):
                copy_x(pair, g, g % 2 == 1)
            for g in range(PASSES):
                quantise_x(pair, g)
            first_exit(0, 2 * (pair - 2))
            first_exit(0, 2 * (pair - 2) + 1)

        for i in range(COL_TILES):
            multiply(1, i)
        turn_back(0, 2)
        turn_back(0, 3)
        regroup_w(1, 0)
        for g in range(1, PASSES):
            regroup_w(1, g)
            quantise_w(1, g - 1)
        quantise_w(1, PASSES - 1)
        for i in range(COL_TILES):
            first_exit(1, i)
        for i in range(COL_TILES):
            second_exit(0, i)
        store(0, 0, COL_TILES)

        def whole_unit(u):
            for i in range(COL_TILES):
                multiply(u, i)
                first_exit(u, i)

        def finish_unit(u):
            for i in range(COL_TILES):
                finish(u, i)
            store(u, 0, COL_TILES)

        for nb in range(1, N_BLOCKS - 1):
            for h in range(2):
                whole_unit(2 * nb + h)
                regroup_w(nb + 1, 2 * h)
                regroup_w(nb + 1, 2 * h + 1)
                quantise_w(nb + 1, 2 * h)
                quantise_w(nb + 1, 2 * h + 1)
            finish_unit(2 * nb - 1)
            finish_unit(2 * nb)

        whole_unit(LAST - 1)
        multiply(LAST, 0)
        first_exit(LAST, 0)
        finish_unit(LAST - 2)
        finish_unit(LAST - 1)
        multiply(LAST, 1)
        first_exit(LAST, 1)
        multiply(LAST, 2)
        first_exit(LAST, 2)
        finish(LAST, 0)
        finish(LAST, 1)
        store(LAST, 0, 2)
        multiply(LAST, 3)
        first_exit(LAST, 3)
        finish(LAST, 2)
        store(LAST, 2, 3)
        finish(LAST, 3)
        store(LAST, 3, COL_TILES)
